import numpy as np
import ml_dtypes


def mxq(x, axis, fmt="e4m3"):
    dtype, down = {"e4m3": (ml_dtypes.float8_e4m3fn, 7), "e5m2": (ml_dtypes.float8_e5m2, 14)}[fmt]
    v = np.moveaxis(np.asarray(x, np.float32).astype(ml_dtypes.bfloat16).astype(np.float64), axis, -1)
    blocks = v.reshape(v.shape[:-1] + (-1, 32))
    amax = np.abs(blocks).max(-1, keepdims=True)
    byte = np.maximum(np.where(amax > 0, np.frexp(amax)[1] - 1 + 127, 0) - down, 1)
    scale = np.exp2(byte - 127.0)
    codes = (blocks / scale).astype(np.float32).astype(dtype).astype(np.float64)
    return np.moveaxis((codes * scale).reshape(v.shape), -1, axis)


WIDE = False


def mx_kscale(k):
    if not WIDE:
        return np.ones(k)
    levels = np.array([10, -10, 5, -5, 0])
    a = np.random.permutation(np.resize(levels, k // 512 * 4)).reshape(k // 512, 4)
    idx = np.arange(k)
    return np.exp2(a[idx // 512, idx % 128 // 32])


BF16 = ml_dtypes.bfloat16


def bf(x):
    return np.asarray(x, np.float32).astype(BF16)


def f64(x):
    return np.asarray(x).astype(np.float64)


E2M1 = np.array([0.0, 0.5, 1.0, 1.5, 2.0, 3.0, 4.0, 6.0, -0.0, -0.5, -1.0, -1.5, -2.0, -3.0, -4.0, -6.0])


def pack_weight(w, fmt):
    k, n = w.shape
    w = f64(bf(w)).reshape(k // 32, 32, n)
    amax = np.abs(w).max(1)
    if fmt == "e4m3":
        byte = np.frexp(amax)[1] - 1 + 127 - 7
    else:
        mant, ex = np.frexp(amax / 6.0)
        byte = np.where(mant > 0.5, ex, ex - 1) + 127
    byte = np.clip(np.where(amax > 0, byte, 1), 1, 254)
    scaled = (w * np.exp2(127.0 - byte)[:, None, :]).reshape(k, n).astype(np.float32)
    by_word = np.ascontiguousarray(scaled.reshape(k // 512, 128, 4, n).transpose(0, 1, 3, 2))
    if fmt == "e4m3":
        words = by_word.astype(ml_dtypes.float8_e4m3fn).view(np.uint8)
    else:
        c = by_word.astype(ml_dtypes.float4_e2m1fn).view(np.uint8) & 0xF
        words = c[..., 0::2] | (c[..., 1::2] << 4)
    return np.ascontiguousarray(words), np.ascontiguousarray(byte.astype(np.uint8).reshape(k // 512, 16, n))


def unpack_weight(words, scales, fmt):
    g, p, n, _ = words.shape
    if fmt == "e4m3":
        vals = np.ascontiguousarray(words).view(ml_dtypes.float8_e4m3fn).astype(np.float64)
    else:
        nib = np.empty((g, p, n, 4), np.uint8)
        nib[..., 0::2] = words & 0xF
        nib[..., 1::2] = words >> 4
        vals = E2M1[nib]
    vals = vals * np.repeat(np.exp2(scales.astype(np.float64) - 127.0), 8, axis=1)[..., None]
    return vals.transpose(0, 1, 3, 2).reshape(g * 512, n)


B, S, H, QD, KD, R = 4, 2048, 512, 128, 128, 128
SCALING = 2.0
FMT = "e4m3"


def setup_inputs():
    s = mx_kscale(H)

    def w(o):
        return pack_weight((np.random.standard_normal((o, H)) / np.sqrt(H) / s[None, :]).T, FMT)

    def xa():
        return bf(np.random.standard_normal((B, S, R)) * 0.6)

    def up(o):
        return bf(np.random.standard_normal((R, o)) * 0.4 / np.sqrt(R))

    def bias(o):
        return bf(np.random.standard_normal(o) * 0.3)

    x = bf(np.random.standard_normal((B, S, H)) * s)
    Wq_words, Wq_scales = w(QD)
    Wk_words, Wk_scales = w(KD)
    Wv_words, Wv_scales = w(KD)
    return {"x": x,
            "Wq_words": Wq_words, "Wq_scales": Wq_scales,
            "Wk_words": Wk_words, "Wk_scales": Wk_scales,
            "Wv_words": Wv_words, "Wv_scales": Wv_scales,
            "bq": bias(QD), "bk": bias(KD), "bv": bias(KD),
            "xa_q": xa(), "xa_k": xa(), "xa_v": xa(),
            "Bq": up(QD), "Bk": up(KD), "Bv": up(KD)}


def lora_proj(xq, W_words, W_scales, b, xa, Bm):
    base = xq @ unpack_weight(W_words, W_scales, FMT)
    delta = f64(xa) @ f64(Bm)
    return base + SCALING * delta + f64(b)


def reference(x, Wq_words, Wq_scales, Wk_words, Wk_scales, Wv_words, Wv_scales, bq, bk, bv, xa_q, xa_k, xa_v, Bq, Bk, Bv):
    xq = mxq(f64(x), 2, "e4m3")
    q = lora_proj(xq, Wq_words, Wq_scales, bq, xa_q, Bq)
    k = lora_proj(xq, Wk_words, Wk_scales, bk, xa_k, Bk)
    v = lora_proj(xq, Wv_words, Wv_scales, bv, xa_v, Bv)
    return q, k, v

@@ -1,0 +1,236 @@
+from contextlib import ExitStack
+
+import concourse.masks as masks
+import concourse.mybir as mybir
+
+F32 = mybir.dt.float32
+BF16 = mybir.dt.bfloat16
+U8 = mybir.dt.uint8
+U32 = mybir.dt.uint32
+I32 = mybir.dt.int32
+FP8X4 = mybir.dt.float8_e4m3fn_x4
+ALU = mybir.AluOpType
+ACT = mybir.ActivationFunctionType
+
+P = 128
+TOKENS = 4 * 2048
+HIDDEN = 512
+RANK = 128
+OUT = 128
+PROJ = 3
+COLS = PROJ * OUT
+PACK = 4
+SCALING = 2.0
+
+TILES = TOKENS // P
+BLOCK = 8
+BLOCKS = TILES // BLOCK
+PAIR = 2
+ROUNDS = TILES // PAIR
+LEAD = 4
+OUT_BUFS = 5
+
+FLOPS = 2 * TOKENS * (HIDDEN + RANK) * COLS
+
+
+def tile_loraqkvlinear_pa_t_kernel(
+    tc,
+    x,
+    Wq_words,
+    Wq_scales,
+    Wk_words,
+    Wk_scales,
+    Wv_words,
+    Wv_scales,
+    bq,
+    bk,
+    bv,
+    xa_q,
+    xa_k,
+    xa_v,
+    Bq,
+    Bk,
+    Bv,
+    out_0,
+    out_1,
+    out_2,
+):
+    nc = tc.nc
+    w_words_in = (Wq_words, Wk_words, Wv_words)
+    w_scales_in = (Wq_scales, Wk_scales, Wv_scales)
+    bias_in = (bq, bk, bv)
+    up_in = (Bq, Bk, Bv)
+
+    x_rows = x.flatten_outer_dims().rearrange("(p j) h -> p j h", j=TILES)
+    xa_rows = [a.flatten_outer_dims().rearrange("(p j) r -> p j r", j=TILES) for a in (xa_q, xa_k, xa_v)]
+    out_rows = [o.flatten_outer_dims().rearrange("(p j) n -> p j n", j=TILES) for o in (out_0, out_1, out_2)]
+
+    with ExitStack() as ctx:
+        consts = ctx.enter_context(tc.tile_pool(name="consts", bufs=1))
+        inputs = ctx.enter_context(tc.tile_pool(name="inputs", bufs=1))
+        work = ctx.enter_context(tc.tile_pool(name="work", bufs=3))
+        psum = ctx.enter_context(tc.psum_pool(name="psum", bufs=2))
+        ctx.enter_context(tc.manual_schedule())
+
+        ident_f32 = consts.tile([P, P], F32, name="ident_f32")
+        ident_bf16 = consts.tile([P, P], BF16, name="ident_bf16")
+        masks.make_identity(nc, ident_bf16[:])
+        masks.make_identity(nc, ident_f32[:])
+
+        w_codes = consts.tile([P, COLS], U32, name="w_codes", align_bytes=64)
+        w_scales = consts.tile([P, COLS], U8, name="w_scales", align_bytes=64)
+        up_sb = consts.tile([P, PROJ, OUT], BF16, name="up_sb")
+        bias_bf16 = consts.tile([P, COLS], BF16, name="bias_bf16")
+        bias = consts.tile([P, COLS], F32, name="bias")
+        nc.vector.memset(w_scales[:].bitcast(I32), 0)
+
+        x_sb = [inputs.tile([P, BLOCK, HIDDEN], BF16, name="x_sb%d" % b) for b in range(BLOCKS)]
+        xa_sb = [
+            [inputs.tile([P, BLOCK, RANK], BF16, name="xa_sb%d_%d" % (s, b)) for b in range(BLOCKS)]
+            for s in range(PROJ)
+        ]
+
+        def load_x(b):
+            nc.sync.dma_start(out=x_sb[b][:], in_=x_rows[:, b * BLOCK : (b + 1) * BLOCK, :])
+
+        def load_xa(b):
+            for s in range(PROJ):
+                nc.sync.dma_start(out=xa_sb[s][b][:], in_=xa_rows[s][:, b * BLOCK : (b + 1) * BLOCK, :])
+
+        load_xa(0)
+        for s in range(PROJ):
+            nc.sync.dma_start(out=up_sb[:, s, :], in_=up_in[s])
+        for s in range(PROJ):
+            nc.sync.dma_start(out=bias_bf16[:, s * OUT : (s + 1) * OUT], in_=bias_in[s].partition_broadcast(P))
+        load_x(0)
+        load_xa(1)
+        for s in range(PROJ):
+            cols = slice(s * OUT, (s + 1) * OUT)
+            nc.sync.dma_start(
+                out=w_codes[:, cols].bitcast(I32),
+                in_=w_words_in[s].rearrange("g p n t -> (g p) (n t)").bitcast(I32),
+            )
+        for s in range(PROJ):
+            cols = slice(s * OUT, (s + 1) * OUT)
+            for quad in range(4):
+                nc.sync.dma_start(
+                    out=w_scales[32 * quad : 32 * quad + 4, cols].bitcast(I32),
+                    in_=w_scales_in[s][0, 4 * quad : 4 * quad + 4, :].bitcast(I32),
+                )
+        for b in range(1, BLOCKS):
+            load_x(b)
+            if b + 1 < BLOCKS:
+                load_xa(b + 1)
+
+        nc.vector.tensor_copy(out=bias[:], in_=bias_bf16[:])
+
+        def where(r, t):
+            return divmod(PAIR * r + t, BLOCK)
+
+        grouped_of = {}
+        codes_of = {}
+        xaT_of = {}
+        update_of = {}
+        out_of = {}
+
+        def transpose_x(r):
+            xT = psum.tile([P, PAIR, 2, P], F32, name="xT")
+            for t in range(PAIR):
+                b, jj = where(r, t)
+                words = x_sb[b][:, jj, :].bitcast(F32)
+                for u in range(2):
+                    nc.tensor.transpose(xT[:, t, u, :], words[:, u : HIDDEN // 2 : 2], ident_f32[:])
+            grouped = work.tile([P, PAIR * P * PACK], BF16, name="grouped", align_bytes=64)
+            nc.scalar.copy(
+                out=grouped[:].bitcast(F32).rearrange("p (t c u) -> p t c u", t=PAIR, u=2),
+                in_=xT[:].rearrange("p t u c -> p t c u"),
+            )
+            grouped_of[r] = grouped
+
+        def quantise_x(r):
+            codes = work.tile([P, PAIR * P], U32, name="codes", align_bytes=64)
+            scales = work.tile([P, PAIR * P], U8, name="scales", align_bytes=64)
+            nc.vector.quantize_mx(out=codes[:].bitcast(FP8X4), scales=scales[:], in_=grouped_of[r][:])
+            codes_of[r] = (codes, scales)
+
+        def transpose_xa(r):
+            xaT_ps = psum.tile([P, PAIR, PROJ, P], BF16, name="xaT_ps")
+            for t in range(PAIR):
+                b, jj = where(r, t)
+                for s in range(PROJ):
+                    nc.tensor.transpose(xaT_ps[:, t, s, :], xa_sb[s][b][:, jj, :], ident_bf16[:])
+            xaT = work.tile([P, PAIR, PROJ, P], BF16, name="xaT")
+            nc.scalar.copy(out=xaT[:], in_=xaT_ps[:])
+            xaT_of[r] = xaT
+
+        def lora(r):
+            xaT = xaT_of[r]
+            for t in range(PAIR):
+                delta = psum.tile([P, COLS], F32, name="delta")
+                for s in range(PROJ):
+                    nc.tensor.matmul(
+                        delta[:, s * OUT : (s + 1) * OUT],
+                        lhsT=xaT[:, t, s, :],
+                        rhs=up_sb[:, s, :],
+                        start=True,
+                        stop=True,
+                    )
+                update = work.tile([P, COLS], F32, name="update%d" % t, bufs=LEAD + 2)
+                if t == 0:
+                    nc.vector.scalar_tensor_tensor(
+                        out=update[:], in0=delta[:], scalar=SCALING, in1=bias[:], op0=ALU.mult, op1=ALU.add
+                    )
+                else:
+                    nc.scalar.activation(out=update[:], in_=delta[:], func=ACT.Copy, scale=SCALING)
+                    nc.gpsimd.tensor_tensor(out=update[:], in0=update[:], in1=bias[:], op=ALU.add)
+                update_of[(r, t)] = update
+
+        def base_and_sum(r):
+            codes, scales = codes_of[r]
+            for t in range(PAIR):
+                b, jj = where(r, t)
+                if jj == 0:
+                    out_of[b] = work.tile([P, PROJ, BLOCK, OUT], F32, name="out_sb", bufs=OUT_BUFS)
+                tokens = slice(t * P, (t + 1) * P)
+                base = psum.tile([P, COLS], F32, name="base")
+                for cols in (slice(0, 2 * OUT), slice(2 * OUT, COLS)):
+                    nc.tensor.matmul_mx(
+                        out=base[:, cols],
+                        lhsT=codes[:, tokens].bitcast(FP8X4),
+                        lhsT_scale=scales[:, tokens],
+                        rhs=w_codes[:, cols].bitcast(FP8X4),
+                        rhs_scale=w_scales[:, cols],
+                        start=True,
+                        stop=True,
+                    )
+                nc.vector.tensor_tensor(
+                    out=out_of[b][:, :, jj, :],
+                    in0=base[:].rearrange("p (s n) -> p s n", s=PROJ),
+                    in1=update_of[(r, t)][:].rearrange("p (s n) -> p s n", s=PROJ),
+                    op=ALU.add,
+                )
+
+        def store(first_tile, count):
+            b, jj = divmod(first_tile, BLOCK)
+            for s in range(PROJ):
+                nc.sync.dma_start(
+                    out=out_rows[s][:, first_tile : first_tile + count, :],
+                    in_=out_of[b][:, s, jj : jj + count, :],
+                )
+
+        for i in range(-LEAD - 1, ROUNDS):
+            if 0 <= i + 1 < ROUNDS:
+                transpose_x(i + 1)
+            if 0 <= i + LEAD + 1 < ROUNDS:
+                transpose_xa(i + LEAD + 1)
+            if 0 <= i + LEAD < ROUNDS:
+                lora(i + LEAD)
+            if 0 <= i + 1 < ROUNDS:
+                quantise_x(i + 1)
+            if i >= 0:
+                base_and_sum(i)
+                done = PAIR * (i + 1)
+                if done > TILES - BLOCK:
+                    store(done - PAIR, PAIR)
+                elif done % BLOCK == 0:
+                    store(done - BLOCK, BLOCK)

@@ -23,14 +23,30 @@ PACK = 4
 SCALING = 2.0
 
 TILES = TOKENS // P
-BLOCK = 8
-BLOCKS = TILES // BLOCK
 PAIR = 2
 ROUNDS = TILES // PAIR
 LEAD = 4
-OUT_BUFS = 5
+AHEAD = 2
+X_PIECE = 8
+XA_PIECE = 16
+OUT_PIECE = 16
+OUT_BUFS = 3
 
 FLOPS = 2 * TOKENS * (HIDDEN + RANK) * COLS
+
+
+def doubling_pieces(first, limit):
+    pieces = []
+    start, count = 0, first
+    while start < TILES:
+        pieces.append((start, count))
+        start += count
+        count = min(start, limit)
+    return pieces
+
+
+def homes(pieces):
+    return [(k, j) for k, (start, count) in enumerate(pieces) for j in range(count)]
 
 
 def tile_loraqkvlinear_pa_t_kernel(
@@ -84,48 +100,63 @@ def tile_loraqkvlinear_pa_t_kernel(
         bias = consts.tile([P, COLS], F32, name="bias")
         nc.vector.memset(w_scales[:].bitcast(I32), 0)
 
-        x_sb = [inputs.tile([P, BLOCK, HIDDEN], BF16, name="x_sb%d" % b) for b in range(BLOCKS)]
+        x_pieces = doubling_pieces(X_PIECE, X_PIECE)
+        xa_pieces = doubling_pieces(X_PIECE, XA_PIECE)
+        out_pieces = [(TILES - start - count, count) for start, count in reversed(doubling_pieces(PAIR, OUT_PIECE))]
+        x_home = homes(x_pieces)
+        xa_home = homes(xa_pieces)
+        out_home = homes(out_pieces)
+
+        x_sb = [inputs.tile([P, count, HIDDEN], BF16, name="x_sb%d" % k) for k, (start, count) in enumerate(x_pieces)]
         xa_sb = [
-            [inputs.tile([P, BLOCK, RANK], BF16, name="xa_sb%d_%d" % (s, b)) for b in range(BLOCKS)]
+            [inputs.tile([P, count, RANK], BF16, name="xa_sb%d_%d" % (s, k)) for k, (start, count) in enumerate(xa_pieces)]
             for s in range(PROJ)
         ]
 
-        def load_x(b):
-            nc.sync.dma_start(out=x_sb[b][:], in_=x_rows[:, b * BLOCK : (b + 1) * BLOCK, :])
+        def load_x(k, queue):
+            start, count = x_pieces[k]
+            queue.dma_start(out=x_sb[k][:], in_=x_rows[:, start : start + count, :])
 
-        def load_xa(b):
+        def load_xa(k, queue):
+            start, count = xa_pieces[k]
             for s in range(PROJ):
-                nc.sync.dma_start(out=xa_sb[s][b][:], in_=xa_rows[s][:, b * BLOCK : (b + 1) * BLOCK, :])
+                queue.dma_start(out=xa_sb[s][k][:], in_=xa_rows[s][:, start : start + count, :])
 
-        load_xa(0)
-        for s in range(PROJ):
-            nc.sync.dma_start(out=up_sb[:, s, :], in_=up_in[s])
-        for s in range(PROJ):
-            nc.sync.dma_start(out=bias_bf16[:, s * OUT : (s + 1) * OUT], in_=bias_in[s].partition_broadcast(P))
-        load_x(0)
-        load_xa(1)
-        for s in range(PROJ):
-            cols = slice(s * OUT, (s + 1) * OUT)
-            nc.sync.dma_start(
-                out=w_codes[:, cols].bitcast(I32),
-                in_=w_words_in[s].rearrange("g p n t -> (g p) (n t)").bitcast(I32),
-            )
-        for s in range(PROJ):
-            cols = slice(s * OUT, (s + 1) * OUT)
-            for quad in range(4):
+        def load_lora_constants():
+            for s in range(PROJ):
+                nc.sync.dma_start(out=up_sb[:, s, :], in_=up_in[s])
+            for s in range(PROJ):
+                nc.sync.dma_start(out=bias_bf16[:, s * OUT : (s + 1) * OUT], in_=bias_in[s].partition_broadcast(P))
+
+        def load_base_weights():
+            for s in range(PROJ):
+                cols = slice(s * OUT, (s + 1) * OUT)
                 nc.sync.dma_start(
-                    out=w_scales[32 * quad : 32 * quad + 4, cols].bitcast(I32),
-                    in_=w_scales_in[s][0, 4 * quad : 4 * quad + 4, :].bitcast(I32),
+                    out=w_codes[:, cols].bitcast(I32),
+                    in_=w_words_in[s].rearrange("g p n t -> (g p) (n t)").bitcast(I32),
                 )
-        for b in range(1, BLOCKS):
-            load_x(b)
-            if b + 1 < BLOCKS:
-                load_xa(b + 1)
+            for s in range(PROJ):
+                cols = slice(s * OUT, (s + 1) * OUT)
+                for quad in range(4):
+                    nc.sync.dma_start(
+                        out=w_scales[32 * quad : 32 * quad + 4, cols].bitcast(I32),
+                        in_=w_scales_in[s][0, 4 * quad : 4 * quad + 4, :].bitcast(I32),
+                    )
+
+        load_xa(0, nc.sync)
+        load_lora_constants()
+        load_xa(1, nc.gpsimd)
+        load_x(0, nc.gpsimd)
+        load_base_weights()
+        xa_loaded = 2
+        for k in range(1, len(x_pieces)):
+            start, count = x_pieces[k]
+            while xa_loaded < len(xa_pieces) and xa_pieces[xa_loaded][0] < start + count + PAIR * LEAD:
+                load_xa(xa_loaded, nc.sync)
+                xa_loaded += 1
+            load_x(k, nc.sync)
 
         nc.vector.tensor_copy(out=bias[:], in_=bias_bf16[:])
-
-        def where(r, t):
-            return divmod(PAIR * r + t, BLOCK)
 
         grouped_of = {}
         codes_of = {}
@@ -136,8 +167,8 @@ def tile_loraqkvlinear_pa_t_kernel(
         def transpose_x(r):
             xT = psum.tile([P, PAIR, 2, P], F32, name="xT")
             for t in range(PAIR):
-                b, jj = where(r, t)
-                words = x_sb[b][:, jj, :].bitcast(F32)
+                k, jj = x_home[PAIR * r + t]
+                words = x_sb[k][:, jj, :].bitcast(F32)
                 for u in range(2):
                     nc.tensor.transpose(xT[:, t, u, :], words[:, u : HIDDEN // 2 : 2], ident_f32[:])
             grouped = work.tile([P, PAIR * P * PACK], BF16, name="grouped", align_bytes=64)
@@ -148,18 +179,18 @@ def tile_loraqkvlinear_pa_t_kernel(
             grouped_of[r] = grouped
 
         def quantise_x(r):
-            codes = work.tile([P, PAIR * P], U32, name="codes", align_bytes=64)
-            scales = work.tile([P, PAIR * P], U8, name="scales", align_bytes=64)
+            codes = work.tile([P, PAIR * P], U32, name="codes", align_bytes=64, bufs=AHEAD + 2)
+            scales = work.tile([P, PAIR * P], U8, name="scales", align_bytes=64, bufs=AHEAD + 2)
             nc.vector.quantize_mx(out=codes[:].bitcast(FP8X4), scales=scales[:], in_=grouped_of[r][:])
             codes_of[r] = (codes, scales)
 
         def transpose_xa(r):
             xaT_ps = psum.tile([P, PAIR, PROJ, P], BF16, name="xaT_ps")
             for t in range(PAIR):
-                b, jj = where(r, t)
+                k, jj = xa_home[PAIR * r + t]
                 for s in range(PROJ):
-                    nc.tensor.transpose(xaT_ps[:, t, s, :], xa_sb[s][b][:, jj, :], ident_bf16[:])
-            xaT = work.tile([P, PAIR, PROJ, P], BF16, name="xaT")
+                    nc.tensor.transpose(xaT_ps[:, t, s, :], xa_sb[s][k][:, jj, :], ident_bf16[:])
+            xaT = work.tile([P, PAIR, PROJ, P], BF16, name="xaT", bufs=AHEAD + 2)
             nc.scalar.copy(out=xaT[:], in_=xaT_ps[:])
             xaT_of[r] = xaT
 
@@ -188,9 +219,9 @@ def tile_loraqkvlinear_pa_t_kernel(
         def base_and_sum(r):
             codes, scales = codes_of[r]
             for t in range(PAIR):
-                b, jj = where(r, t)
+                k, jj = out_home[PAIR * r + t]
                 if jj == 0:
-                    out_of[b] = work.tile([P, PROJ, BLOCK, OUT], F32, name="out_sb", bufs=OUT_BUFS)
+                    out_of[k] = work.tile([P, PROJ, out_pieces[k][1], OUT], F32, name="out_sb", bufs=OUT_BUFS)
                 tokens = slice(t * P, (t + 1) * P)
                 base = psum.tile([P, COLS], F32, name="base")
                 for cols in (slice(0, 2 * OUT), slice(2 * OUT, COLS)):
@@ -204,33 +235,28 @@ def tile_loraqkvlinear_pa_t_kernel(
                         stop=True,
                     )
                 nc.vector.tensor_tensor(
-                    out=out_of[b][:, :, jj, :],
+                    out=out_of[k][:, :, jj, :],
                     in0=base[:].rearrange("p (s n) -> p s n", s=PROJ),
                     in1=update_of[(r, t)][:].rearrange("p (s n) -> p s n", s=PROJ),
                     op=ALU.add,
                 )
 
-        def store(first_tile, count):
-            b, jj = divmod(first_tile, BLOCK)
+        def store(k):
+            start, count = out_pieces[k]
             for s in range(PROJ):
-                nc.sync.dma_start(
-                    out=out_rows[s][:, first_tile : first_tile + count, :],
-                    in_=out_of[b][:, s, jj : jj + count, :],
-                )
+                nc.sync.dma_start(out=out_rows[s][:, start : start + count, :], in_=out_of[k][:, s, :, :])
 
-        for i in range(-LEAD - 1, ROUNDS):
-            if 0 <= i + 1 < ROUNDS:
-                transpose_x(i + 1)
-            if 0 <= i + LEAD + 1 < ROUNDS:
-                transpose_xa(i + LEAD + 1)
+        for i in range(-LEAD - AHEAD, ROUNDS):
+            if 0 <= i + AHEAD < ROUNDS:
+                transpose_x(i + AHEAD)
+            if 0 <= i + LEAD + AHEAD < ROUNDS:
+                transpose_xa(i + LEAD + AHEAD)
             if 0 <= i + LEAD < ROUNDS:
                 lora(i + LEAD)
-            if 0 <= i + 1 < ROUNDS:
-                quantise_x(i + 1)
+            if 0 <= i + AHEAD < ROUNDS:
+                quantise_x(i + AHEAD)
             if i >= 0:
                 base_and_sum(i)
-                done = PAIR * (i + 1)
-                if done > TILES - BLOCK:
-                    store(done - PAIR, PAIR)
-                elif done % BLOCK == 0:
-                    store(done - BLOCK, BLOCK)
+                k, jj = out_home[PAIR * i + PAIR - 1]
+                if jj == out_pieces[k][1] - 1:
+                    store(k)

@@ -23,30 +23,14 @@ PACK = 4
 SCALING = 2.0
 
 TILES = TOKENS // P
+BLOCK = 8
+BLOCKS = TILES // BLOCK
 PAIR = 2
 ROUNDS = TILES // PAIR
 LEAD = 4
-AHEAD = 2
-X_PIECE = 8
-XA_PIECE = 16
-OUT_PIECE = 16
-OUT_BUFS = 3
+OUT_BUFS = 5
 
 FLOPS = 2 * TOKENS * (HIDDEN + RANK) * COLS
-
-
-def doubling_pieces(first, limit):
-    pieces = []
-    start, count = 0, first
-    while start < TILES:
-        pieces.append((start, count))
-        start += count
-        count = min(start, limit)
-    return pieces
-
-
-def homes(pieces):
-    return [(k, j) for k, (start, count) in enumerate(pieces) for j in range(count)]
 
 
 def tile_loraqkvlinear_pa_t_kernel(
@@ -100,75 +84,63 @@ def tile_loraqkvlinear_pa_t_kernel(
         bias = consts.tile([P, COLS], F32, name="bias")
         nc.vector.memset(w_scales[:].bitcast(I32), 0)
 
-        x_pieces = doubling_pieces(X_PIECE, X_PIECE)
-        xa_pieces = doubling_pieces(X_PIECE, XA_PIECE)
-        out_pieces = [(TILES - start - count, count) for start, count in reversed(doubling_pieces(PAIR, OUT_PIECE))]
-        x_home = homes(x_pieces)
-        xa_home = homes(xa_pieces)
-        out_home = homes(out_pieces)
-
-        x_sb = [inputs.tile([P, count, HIDDEN], BF16, name="x_sb%d" % k) for k, (start, count) in enumerate(x_pieces)]
+        x_sb = [inputs.tile([P, BLOCK, HIDDEN], BF16, name="x_sb%d" % b) for b in range(BLOCKS)]
         xa_sb = [
-            [inputs.tile([P, count, RANK], BF16, name="xa_sb%d_%d" % (s, k)) for k, (start, count) in enumerate(xa_pieces)]
+            [inputs.tile([P, BLOCK, RANK], BF16, name="xa_sb%d_%d" % (s, b)) for b in range(BLOCKS)]
             for s in range(PROJ)
         ]
 
-        def load_x(k, queue):
-            start, count = x_pieces[k]
-            queue.dma_start(out=x_sb[k][:], in_=x_rows[:, start : start + count, :])
+        def load_x(b):
+            nc.sync.dma_start(out=x_sb[b][:], in_=x_rows[:, b * BLOCK : (b + 1) * BLOCK, :])
 
-        def load_xa(k, queue):
-            start, count = xa_pieces[k]
+        def load_xa(b):
             for s in range(PROJ):
-                queue.dma_start(out=xa_sb[s][k][:], in_=xa_rows[s][:, start : start + count, :])
+                nc.sync.dma_start(out=xa_sb[s][b][:], in_=xa_rows[s][:, b * BLOCK : (b + 1) * BLOCK, :])
 
-        def load_lora_constants():
-            for s in range(PROJ):
-                nc.sync.dma_start(out=up_sb[:, s, :], in_=up_in[s])
-            for s in range(PROJ):
-                nc.sync.dma_start(out=bias_bf16[:, s * OUT : (s + 1) * OUT], in_=bias_in[s].partition_broadcast(P))
-
-        def load_base_weights():
-            for s in range(PROJ):
-                cols = slice(s * OUT, (s + 1) * OUT)
-                nc.sync.dma_start(
-                    out=w_codes[:, cols].bitcast(I32),
-                    in_=w_words_in[s].rearrange("g p n t -> (g p) (n t)").bitcast(I32),
-                )
-            for s in range(PROJ):
-                cols = slice(s * OUT, (s + 1) * OUT)
-                for quad in range(4):
-                    nc.sync.dma_start(
-                        out=w_scales[32 * quad : 32 * quad + 4, cols].bitcast(I32),
-                        in_=w_scales_in[s][0, 4 * quad : 4 * quad + 4, :].bitcast(I32),
-                    )
-
-        load_xa(0, nc.sync)
-        load_lora_constants()
-        load_xa(1, nc.gpsimd)
-        load_x(0, nc.gpsimd)
-        load_base_weights()
-        xa_loaded = 2
-        for k in range(1, len(x_pieces)):
-            start, count = x_pieces[k]
-            while xa_loaded < len(xa_pieces) and xa_pieces[xa_loaded][0] < start + count + PAIR * LEAD:
-                load_xa(xa_loaded, nc.sync)
-                xa_loaded += 1
-            load_x(k, nc.sync)
+        load_xa(0)
+        for s in range(PROJ):
+            nc.sync.dma_start(out=up_sb[:, s, :], in_=up_in[s])
+        for s in range(PROJ):
+            nc.sync.dma_start(out=bias_bf16[:, s * OUT : (s + 1) * OUT], in_=bias_in[s].partition_broadcast(P))
+        load_x(0)
+        load_xa(1)
+        for s in range(PROJ):
+            cols = slice(s * OUT, (s + 1) * OUT)
+            nc.sync.dma_start(
+                out=w_codes[:, cols].bitcast(I32),
+                in_=w_words_in[s].rearrange("g p n t -> (g p) (n t)").bitcast(I32),
+            )
+        for s in range(PROJ):
+            cols = slice(s * OUT, (s + 1) * OUT)
+            for quad in range(4):
+                plane_rows = w_scales[32 * quad : 32 * quad + 4, cols]
+                given_rows = w_scales_in[s][0, 4 * quad : 4 * quad + 4, :]
+                if s == 0:
+                    nc.sync.dma_start(out=plane_rows.bitcast(I32), in_=given_rows.bitcast(I32))
+                else:
+                    nc.gpsimd.dma_start(out=plane_rows.bitcast(F32), in_=given_rows.bitcast(F32))
+        for b in range(1, BLOCKS):
+            load_x(b)
+            if b + 1 < BLOCKS:
+                load_xa(b + 1)
 
         nc.vector.tensor_copy(out=bias[:], in_=bias_bf16[:])
+
+        def where(r, t):
+            return divmod(PAIR * r + t, BLOCK)
 
         grouped_of = {}
         codes_of = {}
         xaT_of = {}
         update_of = {}
+        base_of = {}
         out_of = {}
 
         def transpose_x(r):
             xT = psum.tile([P, PAIR, 2, P], F32, name="xT")
             for t in range(PAIR):
-                k, jj = x_home[PAIR * r + t]
-                words = x_sb[k][:, jj, :].bitcast(F32)
+                b, jj = where(r, t)
+                words = x_sb[b][:, jj, :].bitcast(F32)
                 for u in range(2):
                     nc.tensor.transpose(xT[:, t, u, :], words[:, u : HIDDEN // 2 : 2], ident_f32[:])
             grouped = work.tile([P, PAIR * P * PACK], BF16, name="grouped", align_bytes=64)
@@ -179,51 +151,46 @@ def tile_loraqkvlinear_pa_t_kernel(
             grouped_of[r] = grouped
 
         def quantise_x(r):
-            codes = work.tile([P, PAIR * P], U32, name="codes", align_bytes=64, bufs=AHEAD + 2)
-            scales = work.tile([P, PAIR * P], U8, name="scales", align_bytes=64, bufs=AHEAD + 2)
+            codes = work.tile([P, PAIR * P], U32, name="codes", align_bytes=64)
+            scales = work.tile([P, PAIR * P], U8, name="scales", align_bytes=64)
             nc.vector.quantize_mx(out=codes[:].bitcast(FP8X4), scales=scales[:], in_=grouped_of[r][:])
             codes_of[r] = (codes, scales)
 
         def transpose_xa(r):
-            xaT_ps = psum.tile([P, PAIR, PROJ, P], BF16, name="xaT_ps")
+            xaT_ps = psum.tile([P, PAIR, PROJ, P], BF16, name="xaT_ps", bufs=1)
             for t in range(PAIR):
-                k, jj = xa_home[PAIR * r + t]
+                b, jj = where(r, t)
                 for s in range(PROJ):
-                    nc.tensor.transpose(xaT_ps[:, t, s, :], xa_sb[s][k][:, jj, :], ident_bf16[:])
-            xaT = work.tile([P, PAIR, PROJ, P], BF16, name="xaT", bufs=AHEAD + 2)
+                    nc.tensor.transpose(xaT_ps[:, t, s, :], xa_sb[s][b][:, jj, :], ident_bf16[:])
+            xaT = work.tile([P, PAIR, PROJ, P], BF16, name="xaT")
             nc.scalar.copy(out=xaT[:], in_=xaT_ps[:])
             xaT_of[r] = xaT
 
-        def lora(r):
-            xaT = xaT_of[r]
-            for t in range(PAIR):
-                delta = psum.tile([P, COLS], F32, name="delta")
-                for s in range(PROJ):
-                    nc.tensor.matmul(
-                        delta[:, s * OUT : (s + 1) * OUT],
-                        lhsT=xaT[:, t, s, :],
-                        rhs=up_sb[:, s, :],
-                        start=True,
-                        stop=True,
-                    )
-                update = work.tile([P, COLS], F32, name="update%d" % t, bufs=LEAD + 2)
-                if t == 0:
-                    nc.vector.scalar_tensor_tensor(
-                        out=update[:], in0=delta[:], scalar=SCALING, in1=bias[:], op0=ALU.mult, op1=ALU.add
-                    )
-                else:
-                    nc.scalar.activation(out=update[:], in_=delta[:], func=ACT.Copy, scale=SCALING)
-                    nc.gpsimd.tensor_tensor(out=update[:], in0=update[:], in1=bias[:], op=ALU.add)
-                update_of[(r, t)] = update
+        def lora(r, t):
+            delta = psum.tile([P, COLS], F32, name="delta")
+            for s in range(PROJ):
+                nc.tensor.matmul(
+                    delta[:, s * OUT : (s + 1) * OUT],
+                    lhsT=xaT_of[r][:, t, s, :],
+                    rhs=up_sb[:, s, :],
+                    start=True,
+                    stop=True,
+                )
+            update = work.tile([P, COLS], F32, name="update%d" % t, bufs=LEAD + 2)
+            if t == 0:
+                nc.vector.scalar_tensor_tensor(
+                    out=update[:], in0=delta[:], scalar=SCALING, in1=bias[:], op0=ALU.mult, op1=ALU.add
+                )
+            else:
+                nc.scalar.activation(out=update[:], in_=delta[:], func=ACT.Copy, scale=SCALING)
+                nc.gpsimd.tensor_tensor(out=update[:], in0=update[:], in1=bias[:], op=ALU.add)
+            update_of[(r, t)] = update
 
-        def base_and_sum(r):
+        def base_products(r):
             codes, scales = codes_of[r]
             for t in range(PAIR):
-                k, jj = out_home[PAIR * r + t]
-                if jj == 0:
-                    out_of[k] = work.tile([P, PROJ, out_pieces[k][1], OUT], F32, name="out_sb", bufs=OUT_BUFS)
                 tokens = slice(t * P, (t + 1) * P)
-                base = psum.tile([P, COLS], F32, name="base")
+                base = psum.tile([P, COLS], F32, name="base", bufs=3)
                 for cols in (slice(0, 2 * OUT), slice(2 * OUT, COLS)):
                     nc.tensor.matmul_mx(
                         out=base[:, cols],
@@ -234,29 +201,45 @@ def tile_loraqkvlinear_pa_t_kernel(
                         start=True,
                         stop=True,
                     )
+                base_of[(r, t)] = base
+
+        def sums(r):
+            for t in range(PAIR):
+                b, jj = where(r, t)
+                if jj == 0:
+                    out_of[b] = work.tile([P, PROJ, BLOCK, OUT], F32, name="out_sb", bufs=OUT_BUFS)
                 nc.vector.tensor_tensor(
-                    out=out_of[k][:, :, jj, :],
-                    in0=base[:].rearrange("p (s n) -> p s n", s=PROJ),
+                    out=out_of[b][:, :, jj, :],
+                    in0=base_of[(r, t)][:].rearrange("p (s n) -> p s n", s=PROJ),
                     in1=update_of[(r, t)][:].rearrange("p (s n) -> p s n", s=PROJ),
                     op=ALU.add,
                 )
 
-        def store(k):
-            start, count = out_pieces[k]
+        def store(first_tile, count):
+            b, jj = divmod(first_tile, BLOCK)
             for s in range(PROJ):
-                nc.sync.dma_start(out=out_rows[s][:, start : start + count, :], in_=out_of[k][:, s, :, :])
+                nc.sync.dma_start(
+                    out=out_rows[s][:, first_tile : first_tile + count, :],
+                    in_=out_of[b][:, s, jj : jj + count, :],
+                )
 
-        for i in range(-LEAD - AHEAD, ROUNDS):
-            if 0 <= i + AHEAD < ROUNDS:
-                transpose_x(i + AHEAD)
-            if 0 <= i + LEAD + AHEAD < ROUNDS:
-                transpose_xa(i + LEAD + AHEAD)
+        for i in range(-LEAD - 1, ROUNDS):
+            if 0 <= i + 1 < ROUNDS:
+                transpose_x(i + 1)
+            if 0 <= i + LEAD + 1 < ROUNDS:
+                transpose_xa(i + LEAD + 1)
             if 0 <= i + LEAD < ROUNDS:
-                lora(i + LEAD)
-            if 0 <= i + AHEAD < ROUNDS:
-                quantise_x(i + AHEAD)
+                lora(i + LEAD, 0)
+            if 0 <= i + 1 < ROUNDS:
+                quantise_x(i + 1)
             if i >= 0:
-                base_and_sum(i)
-                k, jj = out_home[PAIR * i + PAIR - 1]
-                if jj == out_pieces[k][1] - 1:
-                    store(k)
+                base_products(i)
+            if 0 <= i + LEAD < ROUNDS:
+                lora(i + LEAD, 1)
+            if i >= 0:
+                sums(i)
+                done = PAIR * (i + 1)
+                if done > TILES - BLOCK:
+                    store(done - PAIR, PAIR)
+                elif done % BLOCK == 0:
+                    store(done - BLOCK, BLOCK)

@@ -25,10 +25,12 @@ SCALING = 2.0
 TILES = TOKENS // P
 BLOCK = 8
 BLOCKS = TILES // BLOCK
-PAIR = 2
-ROUNDS = TILES // PAIR
-LEAD = 4
+QUAD = 4
+HALF = 2
+STEPS = TILES // QUAD
+LEAD = 2
 OUT_BUFS = 5
+BANKS = 8
 
 FLOPS = 2 * TOKENS * (HIDDEN + RANK) * COLS
 
@@ -68,8 +70,8 @@ def tile_loraqkvlinear_pa_t_kernel(
     with ExitStack() as ctx:
         consts = ctx.enter_context(tc.tile_pool(name="consts", bufs=1))
         inputs = ctx.enter_context(tc.tile_pool(name="inputs", bufs=1))
-        work = ctx.enter_context(tc.tile_pool(name="work", bufs=3))
-        psum = ctx.enter_context(tc.psum_pool(name="psum", bufs=2))
+        work = ctx.enter_context(tc.tile_pool(name="work", bufs=2))
+        psum = ctx.enter_context(tc.psum_pool(name="psum", bufs=BANKS))
         ctx.enter_context(tc.manual_schedule())
 
         ident_f32 = consts.tile([P, P], F32, name="ident_f32")
@@ -80,8 +82,8 @@ def tile_loraqkvlinear_pa_t_kernel(
         w_codes = consts.tile([P, COLS], U32, name="w_codes", align_bytes=64)
         w_scales = consts.tile([P, COLS], U8, name="w_scales", align_bytes=64)
         up_sb = consts.tile([P, PROJ, OUT], BF16, name="up_sb")
-        bias_bf16 = consts.tile([P, COLS], BF16, name="bias_bf16")
-        bias = consts.tile([P, COLS], F32, name="bias")
+        bias_bf16 = consts.tile([P, PROJ, OUT], BF16, name="bias_bf16")
+        bias = consts.tile([P, PROJ, QUAD, OUT], F32, name="bias")
         nc.vector.memset(w_scales[:].bitcast(I32), 0)
 
         x_sb = [inputs.tile([P, BLOCK, HIDDEN], BF16, name="x_sb%d" % b) for b in range(BLOCKS)]
@@ -101,7 +103,7 @@ def tile_loraqkvlinear_pa_t_kernel(
         for s in range(PROJ):
             nc.sync.dma_start(out=up_sb[:, s, :], in_=up_in[s])
         for s in range(PROJ):
-            nc.sync.dma_start(out=bias_bf16[:, s * OUT : (s + 1) * OUT], in_=bias_in[s].partition_broadcast(P))
+            nc.sync.dma_start(out=bias_bf16[:, s, :], in_=bias_in[s].partition_broadcast(P))
         load_x(0)
         load_xa(1)
         for s in range(PROJ):
@@ -124,122 +126,121 @@ def tile_loraqkvlinear_pa_t_kernel(
             if b + 1 < BLOCKS:
                 load_xa(b + 1)
 
-        nc.vector.tensor_copy(out=bias[:], in_=bias_bf16[:])
+        for t in range(QUAD):
+            nc.vector.tensor_copy(out=bias[:, :, t, :], in_=bias_bf16[:])
 
-        def where(r, t):
-            return divmod(PAIR * r + t, BLOCK)
+        def where(i, t):
+            return divmod(QUAD * i + t, BLOCK)
 
         grouped_of = {}
         codes_of = {}
         xaT_of = {}
         update_of = {}
-        base_of = {}
         out_of = {}
 
-        def transpose_x(r):
-            xT = psum.tile([P, PAIR, 2, P], F32, name="xT")
-            for t in range(PAIR):
-                b, jj = where(r, t)
-                words = x_sb[b][:, jj, :].bitcast(F32)
-                for u in range(2):
-                    nc.tensor.transpose(xT[:, t, u, :], words[:, u : HIDDEN // 2 : 2], ident_f32[:])
-            grouped = work.tile([P, PAIR * P * PACK], BF16, name="grouped", align_bytes=64)
-            nc.scalar.copy(
-                out=grouped[:].bitcast(F32).rearrange("p (t c u) -> p t c u", t=PAIR, u=2),
-                in_=xT[:].rearrange("p t u c -> p t c u"),
-            )
-            grouped_of[r] = grouped
+        def transpose_x(i):
+            grouped = work.tile([P, QUAD * P * PACK], BF16, name="grouped", align_bytes=64)
+            for h in range(QUAD // HALF):
+                xT = psum.tile([P, HALF, 2, P], F32, name="bank")
+                for t in range(HALF):
+                    b, jj = where(i, HALF * h + t)
+                    words = x_sb[b][:, jj, :].bitcast(F32)
+                    for u in range(2):
+                        nc.tensor.transpose(xT[:, t, u, :], words[:, u : HIDDEN // 2 : 2], ident_f32[:])
+                part = grouped[:, h * HALF * P * PACK : (h + 1) * HALF * P * PACK]
+                nc.scalar.copy(
+                    out=part.bitcast(F32).rearrange("p (t c u) -> p t c u", t=HALF, u=2),
+                    in_=xT[:].rearrange("p t u c -> p t c u"),
+                )
+            grouped_of[i] = grouped
 
-        def quantise_x(r):
-            codes = work.tile([P, PAIR * P], U32, name="codes", align_bytes=64)
-            scales = work.tile([P, PAIR * P], U8, name="scales", align_bytes=64)
-            nc.vector.quantize_mx(out=codes[:].bitcast(FP8X4), scales=scales[:], in_=grouped_of[r][:])
-            codes_of[r] = (codes, scales)
+        def quantise_x(i):
+            codes = work.tile([P, QUAD * P], U32, name="codes", align_bytes=64)
+            scales = work.tile([P, QUAD * P], U8, name="scales", align_bytes=64)
+            nc.vector.quantize_mx(out=codes[:].bitcast(FP8X4), scales=scales[:], in_=grouped_of[i][:])
+            codes_of[i] = (codes, scales)
 
-        def transpose_xa(r):
-            xaT_ps = psum.tile([P, PAIR, PROJ, P], BF16, name="xaT_ps", bufs=1)
-            for t in range(PAIR):
-                b, jj = where(r, t)
-                for s in range(PROJ):
-                    nc.tensor.transpose(xaT_ps[:, t, s, :], xa_sb[s][b][:, jj, :], ident_bf16[:])
-            xaT = work.tile([P, PAIR, PROJ, P], BF16, name="xaT")
-            nc.scalar.copy(out=xaT[:], in_=xaT_ps[:])
-            xaT_of[r] = xaT
+        def transpose_xa(i):
+            for h in range(QUAD // HALF):
+                xaT_ps = psum.tile([P, HALF, PROJ, P], BF16, name="bank")
+                for t in range(HALF):
+                    b, jj = where(i, HALF * h + t)
+                    for s in range(PROJ):
+                        nc.tensor.transpose(xaT_ps[:, t, s, :], xa_sb[s][b][:, jj, :], ident_bf16[:])
+                xaT = work.tile([P, HALF, PROJ, P], BF16, name="xaT", bufs=5)
+                nc.scalar.copy(
+                    out=xaT[:].rearrange("p t s c -> p (t s c)").bitcast(F32),
+                    in_=xaT_ps[:].rearrange("p t s c -> p (t s c)").bitcast(F32),
+                )
+                xaT_of[(i, h)] = xaT
 
-        def lora(r, t):
-            delta = psum.tile([P, COLS], F32, name="delta")
-            for s in range(PROJ):
+        def lora(i, s):
+            delta = psum.tile([P, QUAD, OUT], F32, name="bank")
+            for t in range(QUAD):
                 nc.tensor.matmul(
-                    delta[:, s * OUT : (s + 1) * OUT],
-                    lhsT=xaT_of[r][:, t, s, :],
+                    delta[:, t, :],
+                    lhsT=xaT_of[(i, t // HALF)][:, t % HALF, s, :],
                     rhs=up_sb[:, s, :],
                     start=True,
                     stop=True,
                 )
-            update = work.tile([P, COLS], F32, name="update%d" % t, bufs=LEAD + 2)
-            if t == 0:
+            update = work.tile([P, QUAD, OUT], F32, name="update", bufs=PROJ * (LEAD + 2))
+            if s == 0 or (s == 2 and i % 2 == 0):
                 nc.vector.scalar_tensor_tensor(
-                    out=update[:], in0=delta[:], scalar=SCALING, in1=bias[:], op0=ALU.mult, op1=ALU.add
+                    out=update[:], in0=delta[:], scalar=SCALING, in1=bias[:, s, :, :], op0=ALU.mult, op1=ALU.add
                 )
             else:
                 nc.scalar.activation(out=update[:], in_=delta[:], func=ACT.Copy, scale=SCALING)
-                nc.gpsimd.tensor_tensor(out=update[:], in0=update[:], in1=bias[:], op=ALU.add)
-            update_of[(r, t)] = update
+                nc.gpsimd.tensor_tensor(out=update[:], in0=update[:], in1=bias[:, s, :, :], op=ALU.add)
+            update_of[(i, s)] = update
 
-        def base_products(r):
-            codes, scales = codes_of[r]
-            for t in range(PAIR):
+        def base_product(i, s):
+            codes, scales = codes_of[i]
+            cols = slice(s * OUT, (s + 1) * OUT)
+            base = psum.tile([P, QUAD, OUT], F32, name="bank")
+            for t in range(QUAD):
                 tokens = slice(t * P, (t + 1) * P)
-                base = psum.tile([P, COLS], F32, name="base", bufs=3)
-                for cols in (slice(0, 2 * OUT), slice(2 * OUT, COLS)):
-                    nc.tensor.matmul_mx(
-                        out=base[:, cols],
-                        lhsT=codes[:, tokens].bitcast(FP8X4),
-                        lhsT_scale=scales[:, tokens],
-                        rhs=w_codes[:, cols].bitcast(FP8X4),
-                        rhs_scale=w_scales[:, cols],
-                        start=True,
-                        stop=True,
-                    )
-                base_of[(r, t)] = base
-
-        def sums(r):
-            for t in range(PAIR):
-                b, jj = where(r, t)
-                if jj == 0:
-                    out_of[b] = work.tile([P, PROJ, BLOCK, OUT], F32, name="out_sb", bufs=OUT_BUFS)
-                nc.vector.tensor_tensor(
-                    out=out_of[b][:, :, jj, :],
-                    in0=base_of[(r, t)][:].rearrange("p (s n) -> p s n", s=PROJ),
-                    in1=update_of[(r, t)][:].rearrange("p (s n) -> p s n", s=PROJ),
-                    op=ALU.add,
+                nc.tensor.matmul_mx(
+                    out=base[:, t, :],
+                    lhsT=codes[:, tokens].bitcast(FP8X4),
+                    lhsT_scale=scales[:, tokens],
+                    rhs=w_codes[:, cols].bitcast(FP8X4),
+                    rhs_scale=w_scales[:, cols],
+                    start=True,
+                    stop=True,
                 )
+            b, jj = where(i, 0)
+            if jj == 0 and s == 0:
+                out_of[b] = work.tile([P, PROJ, BLOCK, OUT], F32, name="out_sb", bufs=OUT_BUFS)
+            nc.vector.tensor_tensor(
+                out=out_of[b][:, s, jj : jj + QUAD, :], in0=base[:], in1=update_of[(i, s)][:], op=ALU.add
+            )
 
-        def store(first_tile, count):
+        def store(s, first_tile, count):
             b, jj = divmod(first_tile, BLOCK)
-            for s in range(PROJ):
-                nc.sync.dma_start(
-                    out=out_rows[s][:, first_tile : first_tile + count, :],
-                    in_=out_of[b][:, s, jj : jj + count, :],
-                )
+            nc.sync.dma_start(
+                out=out_rows[s][:, first_tile : first_tile + count, :],
+                in_=out_of[b][:, s, jj : jj + count, :],
+            )
 
-        for i in range(-LEAD - 1, ROUNDS):
-            if 0 <= i + 1 < ROUNDS:
+        for i in range(-LEAD - 1, STEPS):
+            if 0 <= i + 1 < STEPS:
                 transpose_x(i + 1)
-            if 0 <= i + LEAD + 1 < ROUNDS:
+            if 0 <= i + LEAD + 1 < STEPS:
                 transpose_xa(i + LEAD + 1)
-            if 0 <= i + LEAD < ROUNDS:
-                lora(i + LEAD, 0)
-            if 0 <= i + 1 < ROUNDS:
+            if 0 <= i + 1 < STEPS:
                 quantise_x(i + 1)
+            if 0 <= i + LEAD < STEPS:
+                lora(i + LEAD, 0)
+            last_block = QUAD * i >= TILES - BLOCK
             if i >= 0:
-                base_products(i)
-            if 0 <= i + LEAD < ROUNDS:
+                for s in range(PROJ):
+                    base_product(i, s)
+                    if last_block:
+                        store(s, QUAD * i, QUAD)
+            if 0 <= i + LEAD < STEPS:
                 lora(i + LEAD, 1)
-            if i >= 0:
-                sums(i)
-                done = PAIR * (i + 1)
-                if done > TILES - BLOCK:
-                    store(done - PAIR, PAIR)
-                elif done % BLOCK == 0:
-                    store(done - BLOCK, BLOCK)
+                lora(i + LEAD, 2)
+            if i >= 0 and not last_block and (QUAD * (i + 1)) % BLOCK == 0:
+                for s in range(PROJ):
+                    store(s, QUAD * (i + 1) - BLOCK, BLOCK)

@@ -226,21 +226,19 @@ def tile_loraqkvlinear_pa_t_kernel(
         for i in range(-LEAD - 1, STEPS):
             if 0 <= i + 1 < STEPS:
                 transpose_x(i + 1)
-            if 0 <= i + LEAD + 1 < STEPS:
-                transpose_xa(i + LEAD + 1)
+            if 0 <= i + LEAD < STEPS:
+                for s in range(PROJ):
+                    lora(i + LEAD, s)
             if 0 <= i + 1 < STEPS:
                 quantise_x(i + 1)
-            if 0 <= i + LEAD < STEPS:
-                lora(i + LEAD, 0)
+            if 0 <= i + LEAD + 1 < STEPS:
+                transpose_xa(i + LEAD + 1)
             last_block = QUAD * i >= TILES - BLOCK
             if i >= 0:
                 for s in range(PROJ):
                     base_product(i, s)
                     if last_block:
                         store(s, QUAD * i, QUAD)
-            if 0 <= i + LEAD < STEPS:
-                lora(i + LEAD, 1)
-                lora(i + LEAD, 2)
             if i >= 0 and not last_block and (QUAD * (i + 1)) % BLOCK == 0:
                 for s in range(PROJ):
                     store(s, QUAD * (i + 1) - BLOCK, BLOCK)

@@ -117,10 +117,7 @@ def tile_loraqkvlinear_pa_t_kernel(
             for quad in range(4):
                 plane_rows = w_scales[32 * quad : 32 * quad + 4, cols]
                 given_rows = w_scales_in[s][0, 4 * quad : 4 * quad + 4, :]
-                if s == 0:
-                    nc.sync.dma_start(out=plane_rows.bitcast(I32), in_=given_rows.bitcast(I32))
-                else:
-                    nc.gpsimd.dma_start(out=plane_rows.bitcast(F32), in_=given_rows.bitcast(F32))
+                nc.sync.dma_start(out=plane_rows.bitcast(I32), in_=given_rows.bitcast(I32))
         for b in range(1, BLOCKS):
             load_x(b)
             if b + 1 < BLOCKS:

@@ -31,6 +31,7 @@ STEPS = TILES // QUAD
 LEAD = 2
 OUT_BUFS = 5
 BANKS = 8
+SCALAR_TAKES = 1
 
 FLOPS = 2 * TOKENS * (HIDDEN + RANK) * COLS
 
@@ -132,6 +133,7 @@ def tile_loraqkvlinear_pa_t_kernel(
         grouped_of = {}
         codes_of = {}
         xaT_of = {}
+        delta_of = {}
         update_of = {}
         out_of = {}
 
@@ -171,7 +173,7 @@ def tile_loraqkvlinear_pa_t_kernel(
                 )
                 xaT_of[(i, h)] = xaT
 
-        def lora(i, s):
+        def lora_products(i, s):
             delta = psum.tile([P, QUAD, OUT], F32, name="bank")
             for t in range(QUAD):
                 nc.tensor.matmul(
@@ -181,8 +183,12 @@ def tile_loraqkvlinear_pa_t_kernel(
                     start=True,
                     stop=True,
                 )
+            delta_of[(i, s)] = delta
+
+        def lora_update(i, s):
+            delta = delta_of[(i, s)]
             update = work.tile([P, QUAD, OUT], F32, name="update", bufs=PROJ * (LEAD + 2))
-            if s == 0 or (s == 2 and i % 2 == 0):
+            if s != SCALAR_TAKES:
                 nc.vector.scalar_tensor_tensor(
                     out=update[:], in0=delta[:], scalar=SCALING, in1=bias[:, s, :, :], op0=ALU.mult, op1=ALU.add
                 )
@@ -225,11 +231,15 @@ def tile_loraqkvlinear_pa_t_kernel(
                 transpose_x(i + 1)
             if 0 <= i + LEAD < STEPS:
                 for s in range(PROJ):
-                    lora(i + LEAD, s)
+                    lora_products(i + LEAD, s)
+                    if s != SCALAR_TAKES:
+                        lora_update(i + LEAD, s)
             if 0 <= i + 1 < STEPS:
                 quantise_x(i + 1)
             if 0 <= i + LEAD + 1 < STEPS:
                 transpose_xa(i + LEAD + 1)
+            if 0 <= i + LEAD < STEPS:
+                lora_update(i + LEAD, SCALAR_TAKES)
             last_block = QUAD * i >= TILES - BLOCK
             if i >= 0:
                 for s in range(PROJ):

@@ -31,6 +31,9 @@ STEPS = TILES // QUAD
 LEAD = 2
 OUT_BUFS = 5
 BANKS = 8
+WARM_COLS = 512
+WARM_BEFORE = 4
+WARM_BRIDGE = 2
 SCALAR_TAKES = 1
 
 FLOPS = 2 * TOKENS * (HIDDEN + RANK) * COLS
@@ -86,6 +89,8 @@ def tile_loraqkvlinear_pa_t_kernel(
         bias_bf16 = consts.tile([P, PROJ, OUT], BF16, name="bias_bf16")
         bias = consts.tile([P, PROJ, QUAD, OUT], F32, name="bias")
         nc.vector.memset(w_scales[:].bitcast(I32), 0)
+        idle_in = consts.tile([P, WARM_COLS], BF16, name="idle_in")
+        nc.vector.memset(idle_in[:], 0.0)
 
         x_sb = [inputs.tile([P, BLOCK, HIDDEN], BF16, name="x_sb%d" % b) for b in range(BLOCKS)]
         xa_sb = [
@@ -93,20 +98,28 @@ def tile_loraqkvlinear_pa_t_kernel(
             for s in range(PROJ)
         ]
 
-        def load_x(b):
-            nc.sync.dma_start(out=x_sb[b][:], in_=x_rows[:, b * BLOCK : (b + 1) * BLOCK, :])
+        def load_x(b, first=0, count=BLOCK):
+            nc.sync.dma_start(
+                out=x_sb[b][:, first : first + count, :],
+                in_=x_rows[:, b * BLOCK + first : b * BLOCK + first + count, :],
+            )
 
-        def load_xa(b):
+        def load_xa(b, first=0, count=BLOCK):
             for s in range(PROJ):
-                nc.sync.dma_start(out=xa_sb[s][b][:], in_=xa_rows[s][:, b * BLOCK : (b + 1) * BLOCK, :])
+                nc.sync.dma_start(
+                    out=xa_sb[s][b][:, first : first + count, :],
+                    in_=xa_rows[s][:, b * BLOCK + first : b * BLOCK + first + count, :],
+                )
 
-        load_xa(0)
-        for s in range(PROJ):
-            nc.sync.dma_start(out=up_sb[:, s, :], in_=up_in[s])
+        load_xa(0, 0, QUAD)
         for s in range(PROJ):
             nc.sync.dma_start(out=bias_bf16[:, s, :], in_=bias_in[s].partition_broadcast(P))
-        load_x(0)
+        for s in range(PROJ):
+            nc.sync.dma_start(out=up_sb[:, s, :], in_=up_in[s])
+        load_xa(0, QUAD, QUAD)
+        load_x(0, 0, QUAD)
         load_xa(1)
+        load_x(0, QUAD, QUAD)
         for s in range(PROJ):
             cols = slice(s * OUT, (s + 1) * OUT)
             nc.sync.dma_start(
@@ -118,7 +131,10 @@ def tile_loraqkvlinear_pa_t_kernel(
             for quad in range(4):
                 plane_rows = w_scales[32 * quad : 32 * quad + 4, cols]
                 given_rows = w_scales_in[s][0, 4 * quad : 4 * quad + 4, :]
-                nc.sync.dma_start(out=plane_rows.bitcast(I32), in_=given_rows.bitcast(I32))
+                if s < PROJ - 1:
+                    nc.sync.dma_start(out=plane_rows.bitcast(I32), in_=given_rows.bitcast(I32))
+                else:
+                    nc.gpsimd.dma_start(out=plane_rows.bitcast(F32), in_=given_rows.bitcast(F32))
         for b in range(1, BLOCKS):
             load_x(b)
             if b + 1 < BLOCKS:
@@ -226,6 +242,12 @@ def tile_loraqkvlinear_pa_t_kernel(
                 in_=out_of[b][:, s, jj : jj + count, :],
             )
 
+        def keep_warm(count):
+            idle_out = psum.tile([P, WARM_COLS], F32, name="bank")
+            for k in range(count):
+                nc.tensor.matmul(idle_out[:], lhsT=idle_in[:, 0:P], rhs=idle_in[:], start=True, stop=True)
+
+        keep_warm(WARM_BEFORE)
         for i in range(-LEAD - 1, STEPS):
             if 0 <= i + 1 < STEPS:
                 transpose_x(i + 1)
@@ -238,6 +260,8 @@ def tile_loraqkvlinear_pa_t_kernel(
                 quantise_x(i + 1)
             if 0 <= i + LEAD + 1 < STEPS:
                 transpose_xa(i + LEAD + 1)
+            if i == -LEAD - 1:
+                keep_warm(WARM_BRIDGE)
             if 0 <= i + LEAD < STEPS:
                 lora_update(i + LEAD, SCALAR_TAKES)
             last_block = QUAD * i >= TILES - BLOCK

@@ -34,7 +34,12 @@ BANKS = 8
 WARM_COLS = 512
 WARM_BEFORE = 4
 WARM_BRIDGE = 2
-SCALAR_TAKES = 1
+G_SCALES = 1
+HEADV = 3
+BIAS_PE = True
+FLANK = False
+FINE = 4
+TAIL = 3
 
 FLOPS = 2 * TOKENS * (HIDDEN + RANK) * COLS
 
@@ -78,19 +83,22 @@ def tile_loraqkvlinear_pa_t_kernel(
         psum = ctx.enter_context(tc.psum_pool(name="psum", bufs=BANKS))
         ctx.enter_context(tc.manual_schedule())
 
+        w_codes = consts.tile([P, COLS], U32, name="w_codes", align_bytes=64)
+        w_scales = consts.tile([P, COLS], U8, name="w_scales", align_bytes=64)
+        nc.gpsimd.memset(w_scales[:], 0)
         ident_f32 = consts.tile([P, P], F32, name="ident_f32")
         ident_bf16 = consts.tile([P, P], BF16, name="ident_bf16")
         masks.make_identity(nc, ident_bf16[:])
         masks.make_identity(nc, ident_f32[:])
-
-        w_codes = consts.tile([P, COLS], U32, name="w_codes", align_bytes=64)
-        w_scales = consts.tile([P, COLS], U8, name="w_scales", align_bytes=64)
         up_sb = consts.tile([P, PROJ, OUT], BF16, name="up_sb")
         bias_bf16 = consts.tile([P, PROJ, OUT], BF16, name="bias_bf16")
         bias = consts.tile([P, PROJ, QUAD, OUT], F32, name="bias")
-        nc.vector.memset(w_scales[:].bitcast(I32), 0)
         idle_in = consts.tile([P, WARM_COLS], BF16, name="idle_in")
         nc.vector.memset(idle_in[:], 0.0)
+        ones = consts.tile([P, P], BF16, name="ones")
+        if BIAS_PE:
+            nc.vector.memset(bias_bf16[:], 0.0)
+            nc.vector.memset(ones[:], 1.0)
 
         x_sb = [inputs.tile([P, BLOCK, HIDDEN], BF16, name="x_sb%d" % b) for b in range(BLOCKS)]
         xa_sb = [
@@ -111,54 +119,73 @@ def tile_loraqkvlinear_pa_t_kernel(
                     in_=xa_rows[s][:, b * BLOCK + first : b * BLOCK + first + count, :],
                 )
 
-        load_xa(0, 0, QUAD)
-        for s in range(PROJ):
-            nc.sync.dma_start(out=bias_bf16[:, s, :], in_=bias_in[s].partition_broadcast(P))
-        for s in range(PROJ):
-            nc.sync.dma_start(out=up_sb[:, s, :], in_=up_in[s])
-        load_xa(0, QUAD, QUAD)
-        load_x(0, 0, QUAD)
-        load_xa(1)
-        load_x(0, QUAD, QUAD)
-        for s in range(PROJ):
-            cols = slice(s * OUT, (s + 1) * OUT)
-            nc.sync.dma_start(
-                out=w_codes[:, cols].bitcast(I32),
-                in_=w_words_in[s].rearrange("g p n t -> (g p) (n t)").bitcast(I32),
-            )
-        for s in range(PROJ):
+        def load_codes():
+            for s in range(PROJ):
+                cols = slice(s * OUT, (s + 1) * OUT)
+                nc.sync.dma_start(
+                    out=w_codes[:, cols].bitcast(I32),
+                    in_=w_words_in[s].rearrange("g p n t -> (g p) (n t)").bitcast(I32),
+                )
+
+        def load_scales(s):
             cols = slice(s * OUT, (s + 1) * OUT)
             for quad in range(4):
                 plane_rows = w_scales[32 * quad : 32 * quad + 4, cols]
                 given_rows = w_scales_in[s][0, 4 * quad : 4 * quad + 4, :]
-                if s < PROJ - 1:
+                if s < PROJ - G_SCALES:
                     nc.sync.dma_start(out=plane_rows.bitcast(I32), in_=given_rows.bitcast(I32))
                 else:
                     nc.gpsimd.dma_start(out=plane_rows.bitcast(F32), in_=given_rows.bitcast(F32))
-        for b in range(1, BLOCKS):
+
+        def load_bias(s):
+            if BIAS_PE:
+                nc.sync.dma_start(out=bias_bf16[0:1, s, :], in_=bias_in[s].rearrange("(o n) -> o n", o=1))
+            else:
+                nc.sync.dma_start(out=bias_bf16[:, s, :], in_=bias_in[s].partition_broadcast(P))
+
+        for s in range(PROJ - G_SCALES, PROJ):
+            load_scales(s)
+        load_xa(0, 0, QUAD)
+        for s in range(PROJ):
+            nc.sync.dma_start(out=up_sb[:, s, :], in_=up_in[s])
+        load_x(0, 0, QUAD)
+        for s in reversed(range(PROJ)):
+            load_bias(s)
+        load_xa(0, QUAD, QUAD)
+        load_x(0, QUAD, QUAD)
+        load_xa(1, 0, QUAD)
+        load_x(1, 0, QUAD)
+        load_codes()
+        load_xa(1, QUAD, QUAD)
+        for s in range(PROJ - G_SCALES):
+            load_scales(s)
+        load_x(1, QUAD, QUAD)
+        for b in range(2, BLOCKS):
+            load_xa(b)
             load_x(b)
-            if b + 1 < BLOCKS:
-                load_xa(b + 1)
 
-        for t in range(QUAD):
-            nc.vector.tensor_copy(out=bias[:, :, t, :], in_=bias_bf16[:])
+        def where(j, t):
+            return divmod(QUAD * j + t, BLOCK)
 
-        def where(i, t):
-            return divmod(QUAD * i + t, BLOCK)
+        def scalar_takes(j):
+            if j < HEADV:
+                return ()
+            return (0, 1) if j < STEPS - TAIL else (0,)
 
         grouped_of = {}
         codes_of = {}
         xaT_of = {}
+        xaT_ps_of = {}
         delta_of = {}
         update_of = {}
         out_of = {}
 
-        def transpose_x(i):
+        def transpose_x(j):
             grouped = work.tile([P, QUAD * P * PACK], BF16, name="grouped", align_bytes=64)
             for h in range(QUAD // HALF):
                 xT = psum.tile([P, HALF, 2, P], F32, name="bank")
                 for t in range(HALF):
-                    b, jj = where(i, HALF * h + t)
+                    b, jj = where(j, HALF * h + t)
                     words = x_sb[b][:, jj, :].bitcast(F32)
                     for u in range(2):
                         nc.tensor.transpose(xT[:, t, u, :], words[:, u : HIDDEN // 2 : 2], ident_f32[:])
@@ -167,19 +194,23 @@ def tile_loraqkvlinear_pa_t_kernel(
                     out=part.bitcast(F32).rearrange("p (t c u) -> p t c u", t=HALF, u=2),
                     in_=xT[:].rearrange("p t u c -> p t c u"),
                 )
-            grouped_of[i] = grouped
+            grouped_of[j] = grouped
 
-        def quantise_x(i):
-            codes = work.tile([P, QUAD * P], U32, name="codes", align_bytes=64)
-            scales = work.tile([P, QUAD * P], U8, name="scales", align_bytes=64)
-            nc.vector.quantize_mx(out=codes[:].bitcast(FP8X4), scales=scales[:], in_=grouped_of[i][:])
-            codes_of[i] = (codes, scales)
+        def quantise_x(j):
+            codes = work.tile([P, QUAD * P], U32, name="codes", align_bytes=64, bufs=3)
+            scales = work.tile([P, QUAD * P], U8, name="scales", align_bytes=64, bufs=3)
+            nc.vector.quantize_mx(out=codes[:].bitcast(FP8X4), scales=scales[:], in_=grouped_of[j][:])
+            codes_of[j] = (codes, scales)
 
-        def transpose_xa(i):
+        def xa_banks(j):
             for h in range(QUAD // HALF):
-                xaT_ps = psum.tile([P, HALF, PROJ, P], BF16, name="bank")
+                xaT_ps_of[(j, h)] = psum.tile([P, HALF, PROJ, P], BF16, name="bank")
+
+        def transpose_xa(j):
+            for h in range(QUAD // HALF):
+                xaT_ps = xaT_ps_of[(j, h)]
                 for t in range(HALF):
-                    b, jj = where(i, HALF * h + t)
+                    b, jj = where(j, HALF * h + t)
                     for s in range(PROJ):
                         nc.tensor.transpose(xaT_ps[:, t, s, :], xa_sb[s][b][:, jj, :], ident_bf16[:])
                 xaT = work.tile([P, HALF, PROJ, P], BF16, name="xaT", bufs=5)
@@ -187,34 +218,34 @@ def tile_loraqkvlinear_pa_t_kernel(
                     out=xaT[:].rearrange("p t s c -> p (t s c)").bitcast(F32),
                     in_=xaT_ps[:].rearrange("p t s c -> p (t s c)").bitcast(F32),
                 )
-                xaT_of[(i, h)] = xaT
+                xaT_of[(j, h)] = xaT
 
-        def lora_products(i, s):
-            delta = psum.tile([P, QUAD, OUT], F32, name="bank")
-            for t in range(QUAD):
+        def lora_bank(j, s):
+            delta_of[(j, s)] = psum.tile([P, QUAD, OUT], F32, name="bank")
+
+        def lora_products(j, s, tiles):
+            for t in tiles:
                 nc.tensor.matmul(
-                    delta[:, t, :],
-                    lhsT=xaT_of[(i, t // HALF)][:, t % HALF, s, :],
+                    delta_of[(j, s)][:, t, :],
+                    lhsT=xaT_of[(j, t // HALF)][:, t % HALF, s, :],
                     rhs=up_sb[:, s, :],
                     start=True,
                     stop=True,
                 )
-            delta_of[(i, s)] = delta
 
-        def lora_update(i, s):
-            delta = delta_of[(i, s)]
+        def lora_update(j, s):
+            delta = delta_of[(j, s)]
             update = work.tile([P, QUAD, OUT], F32, name="update", bufs=PROJ * (LEAD + 2))
-            if s != SCALAR_TAKES:
+            if s in scalar_takes(j):
+                nc.scalar.activation(out=update[:], in_=delta[:], func=ACT.Copy, scale=SCALING)
+            else:
                 nc.vector.scalar_tensor_tensor(
                     out=update[:], in0=delta[:], scalar=SCALING, in1=bias[:, s, :, :], op0=ALU.mult, op1=ALU.add
                 )
-            else:
-                nc.scalar.activation(out=update[:], in_=delta[:], func=ACT.Copy, scale=SCALING)
-                nc.gpsimd.tensor_tensor(out=update[:], in0=update[:], in1=bias[:, s, :, :], op=ALU.add)
-            update_of[(i, s)] = update
+            update_of[(j, s)] = update
 
-        def base_product(i, s):
-            codes, scales = codes_of[i]
+        def base_product(j, s):
+            codes, scales = codes_of[j]
             cols = slice(s * OUT, (s + 1) * OUT)
             base = psum.tile([P, QUAD, OUT], F32, name="bank")
             for t in range(QUAD):
@@ -228,12 +259,13 @@ def tile_loraqkvlinear_pa_t_kernel(
                     start=True,
                     stop=True,
                 )
-            b, jj = where(i, 0)
-            if jj == 0 and s == 0:
+            b, jj = where(j, 0)
+            if b not in out_of:
                 out_of[b] = work.tile([P, PROJ, BLOCK, OUT], F32, name="out_sb", bufs=OUT_BUFS)
-            nc.vector.tensor_tensor(
-                out=out_of[b][:, s, jj : jj + QUAD, :], in0=base[:], in1=update_of[(i, s)][:], op=ALU.add
-            )
+            result = out_of[b][:, s, jj : jj + QUAD, :]
+            nc.vector.tensor_tensor(out=result, in0=base[:], in1=update_of[(j, s)][:], op=ALU.add)
+            if s in scalar_takes(j):
+                nc.gpsimd.tensor_tensor(out=result, in0=result, in1=bias[:, s, :, :], op=ALU.add)
 
         def store(s, first_tile, count):
             b, jj = divmod(first_tile, BLOCK)
@@ -247,29 +279,55 @@ def tile_loraqkvlinear_pa_t_kernel(
             for k in range(count):
                 nc.tensor.matmul(idle_out[:], lhsT=idle_in[:, 0:P], rhs=idle_in[:], start=True, stop=True)
 
+        def spread_bias():
+            if BIAS_PE:
+                spread = psum.tile([P, PROJ, OUT], F32, name="bank")
+                nc.tensor.matmul(spread[:].rearrange("p s n -> p (s n)"), lhsT=ones[:], rhs=bias_bf16[:].rearrange("p s n -> p (s n)"), start=True, stop=True)
+                for t in range(QUAD):
+                    nc.vector.tensor_copy(out=bias[:, :, t, :], in_=spread[:])
+            else:
+                for t in range(QUAD):
+                    nc.vector.tensor_copy(out=bias[:, :, t, :], in_=bias_bf16[:])
+
         keep_warm(WARM_BEFORE)
+        LAST = PROJ - 1
         for i in range(-LEAD - 1, STEPS):
-            if 0 <= i + 1 < STEPS:
-                transpose_x(i + 1)
-            if 0 <= i + LEAD < STEPS:
-                for s in range(PROJ):
-                    lora_products(i + LEAD, s)
-                    if s != SCALAR_TAKES:
-                        lora_update(i + LEAD, s)
-            if 0 <= i + 1 < STEPS:
-                quantise_x(i + 1)
-            if 0 <= i + LEAD + 1 < STEPS:
-                transpose_xa(i + LEAD + 1)
+            ahead = i + LEAD
+            if 0 <= ahead < STEPS:
+                transpose_x(ahead)
+                for s in range(PROJ if not FLANK else LAST):
+                    lora_bank(ahead, s)
+                    lora_products(ahead, s, range(QUAD))
+                    lora_update(ahead, s)
+            if 0 <= ahead + 1 < STEPS:
+                xa_banks(ahead + 1)
+            if FLANK and 0 <= ahead < STEPS:
+                lora_bank(ahead, LAST)
+                lora_products(ahead, LAST, range(QUAD - 2))
+            if 0 <= ahead + 1 < STEPS:
+                transpose_xa(ahead + 1)
             if i == -LEAD - 1:
                 keep_warm(WARM_BRIDGE)
-            if 0 <= i + LEAD < STEPS:
-                lora_update(i + LEAD, SCALAR_TAKES)
-            last_block = QUAD * i >= TILES - BLOCK
-            if i >= 0:
-                for s in range(PROJ):
+                spread_bias()
+            if FLANK and 0 <= ahead < STEPS:
+                lora_products(ahead, LAST, [QUAD - 1 - 1])
+            fine = i >= STEPS - FINE
+            late = []
+            for s in range(PROJ):
+                if i >= 0:
                     base_product(i, s)
-                    if last_block:
-                        store(s, QUAD * i, QUAD)
-            if i >= 0 and not last_block and (QUAD * (i + 1)) % BLOCK == 0:
+                    if fine:
+                        if s in scalar_takes(i):
+                            late.append(s)
+                        else:
+                            store(s, QUAD * i, QUAD)
+                if s == 0 and 0 <= ahead < STEPS:
+                    quantise_x(ahead)
+            for s in late:
+                store(s, QUAD * i, QUAD)
+            if FLANK and 0 <= ahead < STEPS:
+                lora_products(ahead, LAST, [QUAD - 1])
+                lora_update(ahead, LAST)
+            if i >= 0 and not fine and (QUAD * (i + 1)) % BLOCK == 0:
                 for s in range(PROJ):
                     store(s, QUAD * (i + 1) - BLOCK, BLOCK)

@@ -19,6 +19,7 @@ RANK = 128
 OUT = 128
 PROJ = 3
 COLS = PROJ * OUT
+PAIR = 2
 PACK = 4
 SCALING = 2.0
 
@@ -38,6 +39,7 @@ G_SCALES = 1
 HEADV = 3
 BIAS_PE = True
 FLANK = False
+DUMMY = 0
 FINE = 4
 TAIL = 3
 
@@ -177,13 +179,19 @@ def tile_loraqkvlinear_pa_t_kernel(
         xaT_of = {}
         xaT_ps_of = {}
         delta_of = {}
-        update_of = {}
+        pair_of = {}
+        last_of = {}
         out_of = {}
 
-        def transpose_x(j):
+        def idle_pass(where_to):
+            nc.tensor.matmul(where_to, lhsT=idle_in[:, 0:P], rhs=idle_in[:, 0:DUMMY], start=True, stop=True)
+
+        def transpose_x(j, after_mx):
             grouped = work.tile([P, QUAD * P * PACK], BF16, name="grouped", align_bytes=64)
             for h in range(QUAD // HALF):
                 xT = psum.tile([P, HALF, 2, P], F32, name="bank")
+                if h == 0 and after_mx and DUMMY:
+                    idle_pass(xT[:, 0, 0, 0:DUMMY])
                 for t in range(HALF):
                     b, jj = where(j, HALF * h + t)
                     words = x_sb[b][:, jj, :].bitcast(F32)
@@ -235,37 +243,70 @@ def tile_loraqkvlinear_pa_t_kernel(
 
         def lora_update(j, s):
             delta = delta_of[(j, s)]
-            update = work.tile([P, QUAD, OUT], F32, name="update", bufs=PROJ * (LEAD + 2))
+            if s == 0:
+                pair_of[j] = work.tile([P, PAIR, QUAD, OUT], F32, name="update_pair", bufs=LEAD + 2)
+            if s < PAIR:
+                update = pair_of[j][:, s, :, :]
+            else:
+                last_of[j] = work.tile([P, QUAD, OUT], F32, name="update_last", bufs=LEAD + 2)
+                update = last_of[j][:]
             if s in scalar_takes(j):
-                nc.scalar.activation(out=update[:], in_=delta[:], func=ACT.Copy, scale=SCALING)
+                nc.scalar.activation(out=update, in_=delta[:], func=ACT.Copy, scale=SCALING)
             else:
                 nc.vector.scalar_tensor_tensor(
-                    out=update[:], in0=delta[:], scalar=SCALING, in1=bias[:, s, :, :], op0=ALU.mult, op1=ALU.add
+                    out=update, in0=delta[:], scalar=SCALING, in1=bias[:, s, :, :], op0=ALU.mult, op1=ALU.add
                 )
-            update_of[(j, s)] = update
 
-        def base_product(j, s):
+        def mx_pass(j, t, out, cols):
             codes, scales = codes_of[j]
-            cols = slice(s * OUT, (s + 1) * OUT)
-            base = psum.tile([P, QUAD, OUT], F32, name="bank")
-            for t in range(QUAD):
-                tokens = slice(t * P, (t + 1) * P)
-                nc.tensor.matmul_mx(
-                    out=base[:, t, :],
-                    lhsT=codes[:, tokens].bitcast(FP8X4),
-                    lhsT_scale=scales[:, tokens],
-                    rhs=w_codes[:, cols].bitcast(FP8X4),
-                    rhs_scale=w_scales[:, cols],
-                    start=True,
-                    stop=True,
-                )
+            tokens = slice(t * P, (t + 1) * P)
+            nc.tensor.matmul_mx(
+                out=out,
+                lhsT=codes[:, tokens].bitcast(FP8X4),
+                lhsT_scale=scales[:, tokens],
+                rhs=w_codes[:, cols].bitcast(FP8X4),
+                rhs_scale=w_scales[:, cols],
+                start=True,
+                stop=True,
+            )
+
+        def results(j):
             b, jj = where(j, 0)
             if b not in out_of:
                 out_of[b] = work.tile([P, PROJ, BLOCK, OUT], F32, name="out_sb", bufs=OUT_BUFS)
-            result = out_of[b][:, s, jj : jj + QUAD, :]
-            nc.vector.tensor_tensor(out=result, in0=base[:], in1=update_of[(j, s)][:], op=ALU.add)
-            if s in scalar_takes(j):
-                nc.gpsimd.tensor_tensor(out=result, in0=result, in1=bias[:, s, :, :], op=ALU.add)
+            return out_of[b], jj
+
+        def base_pair(j, h, after_transposes):
+            base = psum.tile([P, HALF, PAIR, OUT], F32, name="bank")
+            if after_transposes and DUMMY:
+                idle_pass(base[:, 0, 0, 0:DUMMY])
+            for t in range(HALF):
+                mx_pass(j, HALF * h + t, base[:, t, :, :].rearrange("p s n -> p (s n)"), slice(0, PAIR * OUT))
+            out_sb, jj = results(j)
+            first = jj + HALF * h
+            result = out_sb[:, 0:PAIR, first : first + HALF, :]
+            nc.vector.tensor_tensor(
+                out=result,
+                in0=base[:].rearrange("p t s n -> p s t n"),
+                in1=pair_of[j][:, :, HALF * h : HALF * (h + 1), :],
+                op=ALU.add,
+            )
+            late = [s for s in range(PAIR) if s in scalar_takes(j)]
+            if late:
+                some = slice(late[0], late[-1] + 1)
+                nc.gpsimd.tensor_tensor(
+                    out=out_sb[:, some, first : first + HALF, :],
+                    in0=out_sb[:, some, first : first + HALF, :],
+                    in1=bias[:, some, 0:HALF, :],
+                    op=ALU.add,
+                )
+
+        def base_last(j):
+            base = psum.tile([P, QUAD, OUT], F32, name="bank")
+            for t in range(QUAD):
+                mx_pass(j, t, base[:, t, :], slice(PAIR * OUT, COLS))
+            out_sb, jj = results(j)
+            nc.vector.tensor_tensor(out=out_sb[:, PAIR, jj : jj + QUAD, :], in0=base[:], in1=last_of[j][:], op=ALU.add)
 
         def store(s, first_tile, count):
             b, jj = divmod(first_tile, BLOCK)
@@ -294,7 +335,7 @@ def tile_loraqkvlinear_pa_t_kernel(
         for i in range(-LEAD - 1, STEPS):
             ahead = i + LEAD
             if 0 <= ahead < STEPS:
-                transpose_x(ahead)
+                transpose_x(ahead, i >= 1)
                 for s in range(PROJ if not FLANK else LAST):
                     lora_bank(ahead, s)
                     lora_products(ahead, s, range(QUAD))
@@ -312,19 +353,22 @@ def tile_loraqkvlinear_pa_t_kernel(
             if FLANK and 0 <= ahead < STEPS:
                 lora_products(ahead, LAST, [QUAD - 1 - 1])
             fine = i >= STEPS - FINE
-            late = []
-            for s in range(PROJ):
-                if i >= 0:
-                    base_product(i, s)
-                    if fine:
-                        if s in scalar_takes(i):
-                            late.append(s)
-                        else:
+            if i >= 0:
+                base_pair(i, 0, ahead + 1 < STEPS)
+            if 0 <= ahead < STEPS:
+                quantise_x(ahead)
+            if i >= 0:
+                base_pair(i, 1, False)
+                if fine:
+                    for s in range(PAIR):
+                        if s not in scalar_takes(i):
                             store(s, QUAD * i, QUAD)
-                if s == 0 and 0 <= ahead < STEPS:
-                    quantise_x(ahead)
-            for s in late:
-                store(s, QUAD * i, QUAD)
+                base_last(i)
+                if fine:
+                    store(PAIR, QUAD * i, QUAD)
+                    for s in range(PAIR):
+                        if s in scalar_takes(i):
+                            store(s, QUAD * i, QUAD)
             if FLANK and 0 <= ahead < STEPS:
                 lora_products(ahead, LAST, [QUAD - 1])
                 lora_update(ahead, LAST)

@@ -36,6 +36,7 @@ WARM_COLS = 512
 WARM_BEFORE = 4
 WARM_BRIDGE = 2
 G_SCALES = 1
+ALTERNATE = False
 HEADV = 3
 BIAS_PE = True
 FLANK = False
@@ -172,26 +173,34 @@ def tile_loraqkvlinear_pa_t_kernel(
         def scalar_takes(j):
             if j < HEADV:
                 return ()
-            return (0, 1) if j < STEPS - TAIL else (0,)
+            if j >= STEPS - TAIL or (ALTERNATE and j % 2 == 1):
+                return (0,)
+            return (0, 1)
 
+        SHAPES = {
+            "X": ([P, HALF, 2, P], F32),
+            "A": ([P, HALF, PROJ, P], BF16),
+            "L": ([P, QUAD, OUT], F32),
+            "M": ([P, HALF, PAIR, OUT], F32),
+            "V": ([P, QUAD, OUT], F32),
+        }
+        bank_of = {}
         grouped_of = {}
         codes_of = {}
         xaT_of = {}
-        xaT_ps_of = {}
-        delta_of = {}
         pair_of = {}
         last_of = {}
         out_of = {}
 
-        def idle_pass(where_to):
-            nc.tensor.matmul(where_to, lhsT=idle_in[:, 0:P], rhs=idle_in[:, 0:DUMMY], start=True, stop=True)
+        def take(kind, j, n):
+            shape, dtype = SHAPES[kind]
+            bank_of[(kind, j, n)] = psum.tile(shape, dtype, name="bank")
 
-        def transpose_x(j, after_mx):
+        def transpose_x(j):
             grouped = work.tile([P, QUAD * P * PACK], BF16, name="grouped", align_bytes=64)
             for h in range(QUAD // HALF):
-                xT = psum.tile([P, HALF, 2, P], F32, name="bank")
-                if h == 0 and after_mx and DUMMY:
-                    idle_pass(xT[:, 0, 0, 0:DUMMY])
+                take("X", j, h)
+                xT = bank_of[("X", j, h)]
                 for t in range(HALF):
                     b, jj = where(j, HALF * h + t)
                     words = x_sb[b][:, jj, :].bitcast(F32)
@@ -210,13 +219,9 @@ def tile_loraqkvlinear_pa_t_kernel(
             nc.vector.quantize_mx(out=codes[:].bitcast(FP8X4), scales=scales[:], in_=grouped_of[j][:])
             codes_of[j] = (codes, scales)
 
-        def xa_banks(j):
-            for h in range(QUAD // HALF):
-                xaT_ps_of[(j, h)] = psum.tile([P, HALF, PROJ, P], BF16, name="bank")
-
         def transpose_xa(j):
             for h in range(QUAD // HALF):
-                xaT_ps = xaT_ps_of[(j, h)]
+                xaT_ps = bank_of[("A", j, h)]
                 for t in range(HALF):
                     b, jj = where(j, HALF * h + t)
                     for s in range(PROJ):
@@ -228,13 +233,10 @@ def tile_loraqkvlinear_pa_t_kernel(
                 )
                 xaT_of[(j, h)] = xaT
 
-        def lora_bank(j, s):
-            delta_of[(j, s)] = psum.tile([P, QUAD, OUT], F32, name="bank")
-
         def lora_products(j, s, tiles):
             for t in tiles:
                 nc.tensor.matmul(
-                    delta_of[(j, s)][:, t, :],
+                    bank_of[("L", j, s)][:, t, :],
                     lhsT=xaT_of[(j, t // HALF)][:, t % HALF, s, :],
                     rhs=up_sb[:, s, :],
                     start=True,
@@ -242,7 +244,7 @@ def tile_loraqkvlinear_pa_t_kernel(
                 )
 
         def lora_update(j, s):
-            delta = delta_of[(j, s)]
+            delta = bank_of[("L", j, s)]
             if s == 0:
                 pair_of[j] = work.tile([P, PAIR, QUAD, OUT], F32, name="update_pair", bufs=LEAD + 2)
             if s < PAIR:
@@ -270,24 +272,24 @@ def tile_loraqkvlinear_pa_t_kernel(
                 stop=True,
             )
 
+        def base_products(j, h):
+            for t in range(HALF):
+                tile_no = HALF * h + t
+                mx_pass(j, tile_no, bank_of[("M", j, h)][:, t, :, :].rearrange("p s n -> p (s n)"), slice(0, PAIR * OUT))
+                mx_pass(j, tile_no, bank_of[("V", j, 0)][:, tile_no, :], slice(PAIR * OUT, COLS))
+
         def results(j):
             b, jj = where(j, 0)
             if b not in out_of:
                 out_of[b] = work.tile([P, PROJ, BLOCK, OUT], F32, name="out_sb", bufs=OUT_BUFS)
             return out_of[b], jj
 
-        def base_pair(j, h, after_transposes):
-            base = psum.tile([P, HALF, PAIR, OUT], F32, name="bank")
-            if after_transposes and DUMMY:
-                idle_pass(base[:, 0, 0, 0:DUMMY])
-            for t in range(HALF):
-                mx_pass(j, HALF * h + t, base[:, t, :, :].rearrange("p s n -> p (s n)"), slice(0, PAIR * OUT))
+        def finish_pair(j, h):
             out_sb, jj = results(j)
             first = jj + HALF * h
-            result = out_sb[:, 0:PAIR, first : first + HALF, :]
             nc.vector.tensor_tensor(
-                out=result,
-                in0=base[:].rearrange("p t s n -> p s t n"),
+                out=out_sb[:, 0:PAIR, first : first + HALF, :],
+                in0=bank_of[("M", j, h)][:].rearrange("p t s n -> p s t n"),
                 in1=pair_of[j][:, :, HALF * h : HALF * (h + 1), :],
                 op=ALU.add,
             )
@@ -301,12 +303,11 @@ def tile_loraqkvlinear_pa_t_kernel(
                     op=ALU.add,
                 )
 
-        def base_last(j):
-            base = psum.tile([P, QUAD, OUT], F32, name="bank")
-            for t in range(QUAD):
-                mx_pass(j, t, base[:, t, :], slice(PAIR * OUT, COLS))
+        def finish_last(j):
             out_sb, jj = results(j)
-            nc.vector.tensor_tensor(out=out_sb[:, PAIR, jj : jj + QUAD, :], in0=base[:], in1=last_of[j][:], op=ALU.add)
+            nc.vector.tensor_tensor(
+                out=out_sb[:, PAIR, jj : jj + QUAD, :], in0=bank_of[("V", j, 0)][:], in1=last_of[j][:], op=ALU.add
+            )
 
         def store(s, first_tile, count):
             b, jj = divmod(first_tile, BLOCK)
@@ -321,57 +322,74 @@ def tile_loraqkvlinear_pa_t_kernel(
                 nc.tensor.matmul(idle_out[:], lhsT=idle_in[:, 0:P], rhs=idle_in[:], start=True, stop=True)
 
         def spread_bias():
-            if BIAS_PE:
-                spread = psum.tile([P, PROJ, OUT], F32, name="bank")
-                nc.tensor.matmul(spread[:].rearrange("p s n -> p (s n)"), lhsT=ones[:], rhs=bias_bf16[:].rearrange("p s n -> p (s n)"), start=True, stop=True)
-                for t in range(QUAD):
-                    nc.vector.tensor_copy(out=bias[:, :, t, :], in_=spread[:])
-            else:
-                for t in range(QUAD):
-                    nc.vector.tensor_copy(out=bias[:, :, t, :], in_=bias_bf16[:])
+            spread = psum.tile([P, PROJ, OUT], F32, name="bank")
+            nc.tensor.matmul(
+                spread[:].rearrange("p s n -> p (s n)"),
+                lhsT=ones[:],
+                rhs=bias_bf16[:].rearrange("p s n -> p (s n)"),
+                start=True,
+                stop=True,
+            )
+            for t in range(QUAD):
+                nc.vector.tensor_copy(out=bias[:, :, t, :], in_=spread[:])
 
         keep_warm(WARM_BEFORE)
-        LAST = PROJ - 1
         for i in range(-LEAD - 1, STEPS):
             ahead = i + LEAD
-            if 0 <= ahead < STEPS:
-                transpose_x(ahead, i >= 1)
-                for s in range(PROJ if not FLANK else LAST):
-                    lora_bank(ahead, s)
-                    lora_products(ahead, s, range(QUAD))
-                    lora_update(ahead, s)
-            if 0 <= ahead + 1 < STEPS:
-                xa_banks(ahead + 1)
-            if FLANK and 0 <= ahead < STEPS:
-                lora_bank(ahead, LAST)
-                lora_products(ahead, LAST, range(QUAD - 2))
-            if 0 <= ahead + 1 < STEPS:
+            lora = 0 <= ahead < STEPS
+            xa_too = 0 <= ahead + 1 < STEPS
+            base = i >= 0
+            fine = i >= STEPS - FINE
+            if lora:
+                transpose_x(ahead)
+                take("L", ahead, 0)
+            if base:
+                take("M", i, 0)
+            if xa_too:
+                take("A", ahead + 1, 0)
+            if lora:
+                take("L", ahead, 1)
+            if xa_too:
+                take("A", ahead + 1, 1)
+            if base:
+                take("V", i, 0)
+            if lora:
+                lora_products(ahead, 0, (0, 1, 2))
+            if base:
+                base_products(i, 0)
+                finish_pair(i, 0)
+            if lora:
+                quantise_x(ahead)
+                lora_products(ahead, 0, (3,))
+                lora_update(ahead, 0)
+                lora_products(ahead, 1, (0, 1))
+            if xa_too:
                 transpose_xa(ahead + 1)
             if i == -LEAD - 1:
                 keep_warm(WARM_BRIDGE)
                 spread_bias()
-            if FLANK and 0 <= ahead < STEPS:
-                lora_products(ahead, LAST, [QUAD - 1 - 1])
-            fine = i >= STEPS - FINE
-            if i >= 0:
-                base_pair(i, 0, ahead + 1 < STEPS)
-            if 0 <= ahead < STEPS:
-                quantise_x(ahead)
-            if i >= 0:
-                base_pair(i, 1, False)
+            if lora:
+                take("L", ahead, 2)
+                lora_products(ahead, 1, (2, 3))
+                lora_update(ahead, 1)
+                lora_products(ahead, 2, (0,))
+            if base:
+                take("M", i, 1)
+                base_products(i, 1)
+                finish_pair(i, 1)
                 if fine:
                     for s in range(PAIR):
                         if s not in scalar_takes(i):
                             store(s, QUAD * i, QUAD)
-                base_last(i)
+                finish_last(i)
                 if fine:
                     store(PAIR, QUAD * i, QUAD)
                     for s in range(PAIR):
                         if s in scalar_takes(i):
                             store(s, QUAD * i, QUAD)
-            if FLANK and 0 <= ahead < STEPS:
-                lora_products(ahead, LAST, [QUAD - 1])
-                lora_update(ahead, LAST)
-            if i >= 0 and not fine and (QUAD * (i + 1)) % BLOCK == 0:
+            if lora:
+                lora_products(ahead, 2, (1, 2, 3))
+                lora_update(ahead, 2)
+            if base and not fine and (QUAD * (i + 1)) % BLOCK == 0:
                 for s in range(PROJ):
                     store(s, QUAD * (i + 1) - BLOCK, BLOCK)

@@ -36,6 +36,7 @@ WARM_COLS = 512
 WARM_BEFORE = 4
 WARM_BRIDGE = 2
 G_SCALES = 1
+LATE_FIRST = 1
 ALTERNATE = False
 HEADV = 3
 BIAS_PE = True
@@ -355,7 +356,7 @@ def tile_loraqkvlinear_pa_t_kernel(
                 take("V", i, 0)
             if lora:
                 lora_products(ahead, 0, (0, 1, 2))
-            if base:
+            if base and i >= LATE_FIRST:
                 base_products(i, 0)
                 finish_pair(i, 0)
             if lora:
@@ -374,6 +375,9 @@ def tile_loraqkvlinear_pa_t_kernel(
                 lora_update(ahead, 1)
                 lora_products(ahead, 2, (0,))
             if base:
+                if i < LATE_FIRST:
+                    base_products(i, 0)
+                    finish_pair(i, 0)
                 take("M", i, 1)
                 base_products(i, 1)
                 finish_pair(i, 1)

@@ -33,7 +33,7 @@ LEAD = 2
 OUT_BUFS = 5
 BANKS = 8
 WARM_COLS = 512
-WARM_BEFORE = 4
+WARM_BEFORE = 3
 WARM_BRIDGE = 2
 G_SCALES = 1
 LATE_FIRST = 1

from contextlib import ExitStack

import concourse.masks as masks
import concourse.mybir as mybir

F32 = mybir.dt.float32
BF16 = mybir.dt.bfloat16
U8 = mybir.dt.uint8
U32 = mybir.dt.uint32
I32 = mybir.dt.int32
FP8X4 = mybir.dt.float8_e4m3fn_x4
ALU = mybir.AluOpType
ACT = mybir.ActivationFunctionType

P = 128
TOKENS = 4 * 2048
HIDDEN = 512
RANK = 128
OUT = 128
PROJ = 3
COLS = PROJ * OUT
PAIR = 2
PACK = 4
SCALING = 2.0

TILES = TOKENS // P
BLOCK = 8
BLOCKS = TILES // BLOCK
QUAD = 4
HALF = 2
STEPS = TILES // QUAD
LEAD = 2
OUT_BUFS = 5
BANKS = 8
WARM_COLS = 512
WARM_BEFORE = 3
WARM_BRIDGE = 2
G_SCALES = 1
LATE_FIRST = 1
ALTERNATE = False
HEADV = 3
BIAS_PE = True
FLANK = False
DUMMY = 0
FINE = 4
TAIL = 3

FLOPS = 2 * TOKENS * (HIDDEN + RANK) * COLS


def tile_loraqkvlinear_pa_t_kernel(
    tc,
    x,
    Wq_words,
    Wq_scales,
    Wk_words,
    Wk_scales,
    Wv_words,
    Wv_scales,
    bq,
    bk,
    bv,
    xa_q,
    xa_k,
    xa_v,
    Bq,
    Bk,
    Bv,
    out_0,
    out_1,
    out_2,
):
    nc = tc.nc
    w_words_in = (Wq_words, Wk_words, Wv_words)
    w_scales_in = (Wq_scales, Wk_scales, Wv_scales)
    bias_in = (bq, bk, bv)
    up_in = (Bq, Bk, Bv)

    x_rows = x.flatten_outer_dims().rearrange("(p j) h -> p j h", j=TILES)
    xa_rows = [a.flatten_outer_dims().rearrange("(p j) r -> p j r", j=TILES) for a in (xa_q, xa_k, xa_v)]
    out_rows = [o.flatten_outer_dims().rearrange("(p j) n -> p j n", j=TILES) for o in (out_0, out_1, out_2)]

    with ExitStack() as ctx:
        consts = ctx.enter_context(tc.tile_pool(name="consts", bufs=1))
        inputs = ctx.enter_context(tc.tile_pool(name="inputs", bufs=1))
        work = ctx.enter_context(tc.tile_pool(name="work", bufs=2))
        psum = ctx.enter_context(tc.psum_pool(name="psum", bufs=BANKS))
        ctx.enter_context(tc.manual_schedule())

        w_codes = consts.tile([P, COLS], U32, name="w_codes", align_bytes=64)
        w_scales = consts.tile([P, COLS], U8, name="w_scales", align_bytes=64)
        nc.gpsimd.memset(w_scales[:], 0)
        ident_f32 = consts.tile([P, P], F32, name="ident_f32")
        ident_bf16 = consts.tile([P, P], BF16, name="ident_bf16")
        masks.make_identity(nc, ident_bf16[:])
        masks.make_identity(nc, ident_f32[:])
        up_sb = consts.tile([P, PROJ, OUT], BF16, name="up_sb")
        bias_bf16 = consts.tile([P, PROJ, OUT], BF16, name="bias_bf16")
        bias = consts.tile([P, PROJ, QUAD, OUT], F32, name="bias")
        idle_in = consts.tile([P, WARM_COLS], BF16, name="idle_in")
        nc.vector.memset(idle_in[:], 0.0)
        ones = consts.tile([P, P], BF16, name="ones")
        if BIAS_PE:
            nc.vector.memset(bias_bf16[:], 0.0)
            nc.vector.memset(ones[:], 1.0)

        x_sb = [inputs.tile([P, BLOCK, HIDDEN], BF16, name="x_sb%d" % b) for b in range(BLOCKS)]
        xa_sb = [
            [inputs.tile([P, BLOCK, RANK], BF16, name="xa_sb%d_%d" % (s, b)) for b in range(BLOCKS)]
            for s in range(PROJ)
        ]

        def load_x(b, first=0, count=BLOCK):
            nc.sync.dma_start(
                out=x_sb[b][:, first : first + count, :],
                in_=x_rows[:, b * BLOCK + first : b * BLOCK + first + count, :],
            )

        def load_xa(b, first=0, count=BLOCK):
            for s in range(PROJ):
                nc.sync.dma_start(
                    out=xa_sb[s][b][:, first : first + count, :],
                    in_=xa_rows[s][:, b * BLOCK + first : b * BLOCK + first + count, :],
                )

        def load_codes():
            for s in range(PROJ):
                cols = slice(s * OUT, (s + 1) * OUT)
                nc.sync.dma_start(
                    out=w_codes[:, cols].bitcast(I32),
                    in_=w_words_in[s].rearrange("g p n t -> (g p) (n t)").bitcast(I32),
                )

        def load_scales(s):
            cols = slice(s * OUT, (s + 1) * OUT)
            for quad in range(4):
                plane_rows = w_scales[32 * quad : 32 * quad + 4, cols]
                given_rows = w_scales_in[s][0, 4 * quad : 4 * quad + 4, :]
                if s < PROJ - G_SCALES:
                    nc.sync.dma_start(out=plane_rows.bitcast(I32), in_=given_rows.bitcast(I32))
                else:
                    nc.gpsimd.dma_start(out=plane_rows.bitcast(F32), in_=given_rows.bitcast(F32))

        def load_bias(s):
            if BIAS_PE:
                nc.sync.dma_start(out=bias_bf16[0:1, s, :], in_=bias_in[s].rearrange("(o n) -> o n", o=1))
            else:
                nc.sync.dma_start(out=bias_bf16[:, s, :], in_=bias_in[s].partition_broadcast(P))

        for s in range(PROJ - G_SCALES, PROJ):
            load_scales(s)
        load_xa(0, 0, QUAD)
        for s in range(PROJ):
            nc.sync.dma_start(out=up_sb[:, s, :], in_=up_in[s])
        load_x(0, 0, QUAD)
        for s in reversed(range(PROJ)):
            load_bias(s)
        load_xa(0, QUAD, QUAD)
        load_x(0, QUAD, QUAD)
        load_xa(1, 0, QUAD)
        load_x(1, 0, QUAD)
        load_codes()
        load_xa(1, QUAD, QUAD)
        for s in range(PROJ - G_SCALES):
            load_scales(s)
        load_x(1, QUAD, QUAD)
        for b in range(2, BLOCKS):
            load_xa(b)
            load_x(b)

        def where(j, t):
            return divmod(QUAD * j + t, BLOCK)

        def scalar_takes(j):
            if j < HEADV:
                return ()
            if j >= STEPS - TAIL or (ALTERNATE and j % 2 == 1):
                return (0,)
            return (0, 1)

        SHAPES = {
            "X": ([P, HALF, 2, P], F32),
            "A": ([P, HALF, PROJ, P], BF16),
            "L": ([P, QUAD, OUT], F32),
            "M": ([P, HALF, PAIR, OUT], F32),
            "V": ([P, QUAD, OUT], F32),
        }
        bank_of = {}
        grouped_of = {}
        codes_of = {}
        xaT_of = {}
        pair_of = {}
        last_of = {}
        out_of = {}

        def take(kind, j, n):
            shape, dtype = SHAPES[kind]
            bank_of[(kind, j, n)] = psum.tile(shape, dtype, name="bank")

        def transpose_x(j):
            grouped = work.tile([P, QUAD * P * PACK], BF16, name="grouped", align_bytes=64)
            for h in range(QUAD // HALF):
                take("X", j, h)
                xT = bank_of[("X", j, h)]
                for t in range(HALF):
                    b, jj = where(j, HALF * h + t)
                    words = x_sb[b][:, jj, :].bitcast(F32)
                    for u in range(2):
                        nc.tensor.transpose(xT[:, t, u, :], words[:, u : HIDDEN // 2 : 2], ident_f32[:])
                part = grouped[:, h * HALF * P * PACK : (h + 1) * HALF * P * PACK]
                nc.scalar.copy(
                    out=part.bitcast(F32).rearrange("p (t c u) -> p t c u", t=HALF, u=2),
                    in_=xT[:].rearrange("p t u c -> p t c u"),
                )
            grouped_of[j] = grouped

        def quantise_x(j):
            codes = work.tile([P, QUAD * P], U32, name="codes", align_bytes=64, bufs=3)
            scales = work.tile([P, QUAD * P], U8, name="scales", align_bytes=64, bufs=3)
            nc.vector.quantize_mx(out=codes[:].bitcast(FP8X4), scales=scales[:], in_=grouped_of[j][:])
            codes_of[j] = (codes, scales)

        def transpose_xa(j):
            for h in range(QUAD // HALF):
                xaT_ps = bank_of[("A", j, h)]
                for t in range(HALF):
                    b, jj = where(j, HALF * h + t)
                    for s in range(PROJ):
                        nc.tensor.transpose(xaT_ps[:, t, s, :], xa_sb[s][b][:, jj, :], ident_bf16[:])
                xaT = work.tile([P, HALF, PROJ, P], BF16, name="xaT", bufs=5)
                nc.scalar.copy(
                    out=xaT[:].rearrange("p t s c -> p (t s c)").bitcast(F32),
                    in_=xaT_ps[:].rearrange("p t s c -> p (t s c)").bitcast(F32),
                )
                xaT_of[(j, h)] = xaT

        def lora_products(j, s, tiles):
            for t in tiles:
                nc.tensor.matmul(
                    bank_of[("L", j, s)][:, t, :],
                    lhsT=xaT_of[(j, t // HALF)][:, t % HALF, s, :],
                    rhs=up_sb[:, s, :],
                    start=True,
                    stop=True,
                )

        def lora_update(j, s):
            delta = bank_of[("L", j, s)]
            if s == 0:
                pair_of[j] = work.tile([P, PAIR, QUAD, OUT], F32, name="update_pair", bufs=LEAD + 2)
            if s < PAIR:
                update = pair_of[j][:, s, :, :]
            else:
                last_of[j] = work.tile([P, QUAD, OUT], F32, name="update_last", bufs=LEAD + 2)
                update = last_of[j][:]
            if s in scalar_takes(j):
                nc.scalar.activation(out=update, in_=delta[:], func=ACT.Copy, scale=SCALING)
            else:
                nc.vector.scalar_tensor_tensor(
                    out=update, in0=delta[:], scalar=SCALING, in1=bias[:, s, :, :], op0=ALU.mult, op1=ALU.add
                )

        def mx_pass(j, t, out, cols):
            codes, scales = codes_of[j]
            tokens = slice(t * P, (t + 1) * P)
            nc.tensor.matmul_mx(
                out=out,
                lhsT=codes[:, tokens].bitcast(FP8X4),
                lhsT_scale=scales[:, tokens],
                rhs=w_codes[:, cols].bitcast(FP8X4),
                rhs_scale=w_scales[:, cols],
                start=True,
                stop=True,
            )

        def base_products(j, h):
            for t in range(HALF):
                tile_no = HALF * h + t
                mx_pass(j, tile_no, bank_of[("M", j, h)][:, t, :, :].rearrange("p s n -> p (s n)"), slice(0, PAIR * OUT))
                mx_pass(j, tile_no, bank_of[("V", j, 0)][:, tile_no, :], slice(PAIR * OUT, COLS))

        def results(j):
            b, jj = where(j, 0)
            if b not in out_of:
                out_of[b] = work.tile([P, PROJ, BLOCK, OUT], F32, name="out_sb", bufs=OUT_BUFS)
            return out_of[b], jj

        def finish_pair(j, h):
            out_sb, jj = results(j)
            first = jj + HALF * h
            nc.vector.tensor_tensor(
                out=out_sb[:, 0:PAIR, first : first + HALF, :],
                in0=bank_of[("M", j, h)][:].rearrange("p t s n -> p s t n"),
                in1=pair_of[j][:, :, HALF * h : HALF * (h + 1), :],
                op=ALU.add,
            )
            late = [s for s in range(PAIR) if s in scalar_takes(j)]
            if late:
                some = slice(late[0], late[-1] + 1)
                nc.gpsimd.tensor_tensor(
                    out=out_sb[:, some, first : first + HALF, :],
                    in0=out_sb[:, some, first : first + HALF, :],
                    in1=bias[:, some, 0:HALF, :],
                    op=ALU.add,
                )

        def finish_last(j):
            out_sb, jj = results(j)
            nc.vector.tensor_tensor(
                out=out_sb[:, PAIR, jj : jj + QUAD, :], in0=bank_of[("V", j, 0)][:], in1=last_of[j][:], op=ALU.add
            )

        def store(s, first_tile, count):
            b, jj = divmod(first_tile, BLOCK)
            nc.sync.dma_start(
                out=out_rows[s][:, first_tile : first_tile + count, :],
                in_=out_of[b][:, s, jj : jj + count, :],
            )

        def keep_warm(count):
            idle_out = psum.tile([P, WARM_COLS], F32, name="bank")
            for k in range(count):
                nc.tensor.matmul(idle_out[:], lhsT=idle_in[:, 0:P], rhs=idle_in[:], start=True, stop=True)

        def spread_bias():
            spread = psum.tile([P, PROJ, OUT], F32, name="bank")
            nc.tensor.matmul(
                spread[:].rearrange("p s n -> p (s n)"),
                lhsT=ones[:],
                rhs=bias_bf16[:].rearrange("p s n -> p (s n)"),
                start=True,
                stop=True,
            )
            for t in range(QUAD):
                nc.vector.tensor_copy(out=bias[:, :, t, :], in_=spread[:])

        keep_warm(WARM_BEFORE)
        for i in range(-LEAD - 1, STEPS):
            ahead = i + LEAD
            lora = 0 <= ahead < STEPS
            xa_too = 0 <= ahead + 1 < STEPS
            base = i >= 0
            fine = i >= STEPS - FINE
            if lora:
                transpose_x(ahead)
                take("L", ahead, 0)
            if base:
                take("M", i, 0)
            if xa_too:
                take("A", ahead + 1, 0)
            if lora:
                take("L", ahead, 1)
            if xa_too:
                take("A", ahead + 1, 1)
            if base:
                take("V", i, 0)
            if lora:
                lora_products(ahead, 0, (0, 1, 2))
            if base and i >= LATE_FIRST:
                base_products(i, 0)
                finish_pair(i, 0)
            if lora:
                quantise_x(ahead)
                lora_products(ahead, 0, (3,))
                lora_update(ahead, 0)
                lora_products(ahead, 1, (0, 1))
            if xa_too:
                transpose_xa(ahead + 1)
            if i == -LEAD - 1:
                keep_warm(WARM_BRIDGE)
                spread_bias()
            if lora:
                take("L", ahead, 2)
                lora_products(ahead, 1, (2, 3))
                lora_update(ahead, 1)
                lora_products(ahead, 2, (0,))
            if base:
                if i < LATE_FIRST:
                    base_products(i, 0)
                    finish_pair(i, 0)
                take("M", i, 1)
                base_products(i, 1)
                finish_pair(i, 1)
                if fine:
                    for s in range(PAIR):
                        if s not in scalar_takes(i):
                            store(s, QUAD * i, QUAD)
                finish_last(i)
                if fine:
                    store(PAIR, QUAD * i, QUAD)
                    for s in range(PAIR):
                        if s in scalar_takes(i):
                            store(s, QUAD * i, QUAD)
            if lora:
                lora_products(ahead, 2, (1, 2, 3))
                lora_update(ahead, 2)
            if base and not fine and (QUAD * (i + 1)) % BLOCK == 0:
                for s in range(PROJ):
                    store(s, QUAD * (i + 1) - BLOCK, BLOCK)
